import numpy as np
import ml_dtypes


def mxq(x, axis, fmt="e4m3"):
    dtype, down = {"e4m3": (ml_dtypes.float8_e4m3fn, 7), "e5m2": (ml_dtypes.float8_e5m2, 14)}[fmt]
    v = np.moveaxis(np.asarray(x, np.float32).astype(ml_dtypes.bfloat16).astype(np.float64), axis, -1)
    blocks = v.reshape(v.shape[:-1] + (-1, 32))
    amax = np.abs(blocks).max(-1, keepdims=True)
    byte = np.maximum(np.where(amax > 0, np.frexp(amax)[1] - 1 + 127, 0) - down, 1)
    scale = np.exp2(byte - 127.0)
    codes = (blocks / scale).astype(np.float32).astype(dtype).astype(np.float64)
    return np.moveaxis((codes * scale).reshape(v.shape), -1, axis)


WIDE = False


def mx_kscale(k):
    if not WIDE:
        return np.ones(k)
    levels = np.array([10, -10, 5, -5, 0])
    a = np.random.permutation(np.resize(levels, k // 512 * 4)).reshape(k // 512, 4)
    idx = np.arange(k)
    return np.exp2(a[idx // 512, idx % 128 // 32])


BF16 = ml_dtypes.bfloat16


def bf(x):
    return np.asarray(x, np.float32).astype(BF16)


def f64(x):
    return np.asarray(x).astype(np.float64)


E2M1 = np.array([0.0, 0.5, 1.0, 1.5, 2.0, 3.0, 4.0, 6.0, -0.0, -0.5, -1.0, -1.5, -2.0, -3.0, -4.0, -6.0])


def pack_weight(w, fmt):
    k, n = w.shape
    w = f64(bf(w)).reshape(k // 32, 32, n)
    amax = np.abs(w).max(1)
    if fmt == "e4m3":
        byte = np.frexp(amax)[1] - 1 + 127 - 7
    else:
        mant, ex = np.frexp(amax / 6.0)
        byte = np.where(mant > 0.5, ex, ex - 1) + 127
    byte = np.clip(np.where(amax > 0, byte, 1), 1, 254)
    scaled = (w * np.exp2(127.0 - byte)[:, None, :]).reshape(k, n).astype(np.float32)
    by_word = np.ascontiguousarray(scaled.reshape(k // 512, 128, 4, n).transpose(0, 1, 3, 2))
    if fmt == "e4m3":
        words = by_word.astype(ml_dtypes.float8_e4m3fn).view(np.uint8)
    else:
        c = by_word.astype(ml_dtypes.float4_e2m1fn).view(np.uint8) & 0xF
        words = c[..., 0::2] | (c[..., 1::2] << 4)
    return np.ascontiguousarray(words), np.ascontiguousarray(byte.astype(np.uint8).reshape(k // 512, 16, n))


def unpack_weight(words, scales, fmt):
    g, p, n, _ = words.shape
    if fmt == "e4m3":
        vals = np.ascontiguousarray(words).view(ml_dtypes.float8_e4m3fn).astype(np.float64)
    else:
        nib = np.empty((g, p, n, 4), np.uint8)
        nib[..., 0::2] = words & 0xF
        nib[..., 1::2] = words >> 4
        vals = E2M1[nib]
    vals = vals * np.repeat(np.exp2(scales.astype(np.float64) - 127.0), 8, axis=1)[..., None]
    return vals.transpose(0, 1, 3, 2).reshape(g * 512, n)


B, S, D, N = 128, 64, 1024, 256
EPS = 1e-5
FMT = "e4m3"


def batch_bn(x, g, b):
    m = x.mean(axis=0)
    v = x.var(axis=0)
    return g * (x - m) / np.sqrt(v + EPS) + b


def setup_inputs():
    t, u = mx_kscale(D), mx_kscale(D)
    s_z2 = bf(np.random.standard_normal((B, S, D)) * 0.6 + np.random.standard_normal(D) * 0.4)
    c_z2 = bf(np.random.standard_normal((B, D)) * 0.6 + np.random.standard_normal(D) * 0.4)
    s_g2 = bf((1.0 + 0.1 * np.random.standard_normal(D)) * t)
    s_be2 = bf(0.1 * np.random.standard_normal(D) * t)
    s_w3 = np.random.standard_normal((N, D)) * np.sqrt(2.0 / D) / t[None, :]
    s_w3_words, s_w3_scales = pack_weight(np.ascontiguousarray(s_w3.T), FMT)
    s_b3 = bf(0.1 * np.random.standard_normal(N))
    c_g2 = bf((1.0 + 0.1 * np.random.standard_normal(D)) * u)
    c_be2 = bf(0.1 * np.random.standard_normal(D) * u)
    c_w3 = np.random.standard_normal((N, D)) * np.sqrt(2.0 / D) / u[None, :]
    c_w3_words, c_w3_scales = pack_weight(np.ascontiguousarray(c_w3.T), FMT)
    c_b3 = bf(0.1 * np.random.standard_normal(N))
    return {"s_z2": s_z2,
            "c_z2": c_z2,
            "s_g2": s_g2,
            "s_be2": s_be2,
            "s_w3_words": s_w3_words,
            "s_w3_scales": s_w3_scales,
            "s_b3": s_b3,
            "c_g2": c_g2,
            "c_be2": c_be2,
            "c_w3_words": c_w3_words,
            "c_w3_scales": c_w3_scales,
            "c_b3": c_b3}


def reference(s_z2, c_z2, s_g2, s_be2, s_w3_words, s_w3_scales, s_b3, c_g2, c_be2, c_w3_words, c_w3_scales, c_b3):
    c_h = np.maximum(batch_bn(f64(c_z2), f64(c_g2), f64(c_be2)), 0.0)
    c_out = (mxq(c_h, 1, "e4m3") @ unpack_weight(c_w3_words, c_w3_scales, FMT)) + f64(c_b3)
    s_h = np.maximum(batch_bn(f64(s_z2), f64(s_g2), f64(s_be2)), 0.0)
    s_p = (mxq(s_h, 2, "e4m3") @ unpack_weight(s_w3_words, s_w3_scales, FMT)) + f64(s_b3)
    s_out = s_p * c_out[:, None, :]
    aggregated_c = s_out.max(axis=1)
    return (s_out, aggregated_c)

@@ -1,0 +1,255 @@
+from contextlib import ExitStack
+
+import concourse.mybir as mybir
+from concourse.masks import make_identity
+
+F32 = mybir.dt.float32
+BF16 = mybir.dt.bfloat16
+I32 = mybir.dt.int32
+U32 = mybir.dt.uint32
+U8 = mybir.dt.uint8
+FP8X4 = mybir.dt.float8_e4m3fn_x4
+ALU = mybir.AluOpType
+FUNC = mybir.ActivationFunctionType
+
+P = 128
+B, S, D, N = 128, 64, 1024, 256
+EPS = 1e-5
+PACK = 4
+PASSES = D // (P * PACK)
+CHUNKS = PASSES * PACK
+UNIT = 2
+LOAD_SLICES = 4
+QUADRANTS = 4
+VECTOR_PIECE = 3
+
+FLOPS = 2 * (B * S + B) * D * N
+
+
+def tile_cgblock_pb_t_kernel(
+    tc,
+    s_z2,
+    c_z2,
+    s_g2,
+    s_be2,
+    s_w3_words,
+    s_w3_scales,
+    s_b3,
+    c_g2,
+    c_be2,
+    c_w3_words,
+    c_w3_scales,
+    c_b3,
+    out_0,
+    out_1,
+):
+    nc = tc.nc
+    with ExitStack() as ctx:
+        const = ctx.enter_context(tc.tile_pool(name="const", bufs=1))
+        z_pool = ctx.enter_context(tc.tile_pool(name="z", bufs=S // LOAD_SLICES))
+        small = ctx.enter_context(tc.tile_pool(name="small", bufs=3))
+        work_pool = ctx.enter_context(tc.tile_pool(name="work", bufs=2))
+        out_pool = ctx.enter_context(tc.tile_pool(name="out", bufs=3))
+        zt_pool = ctx.enter_context(tc.psum_pool(name="zt", bufs=3 * UNIT))
+        acc_pool = ctx.enter_context(tc.psum_pool(name="acc", bufs=2))
+
+        def load_weight(words, scales, label):
+            codes = const.tile([P, PASSES, N], U32, name=label + "_codes", align_bytes=64)
+            nc.sync.dma_start(
+                out=codes[:].bitcast(I32),
+                in_=words.rearrange("g p n t -> p g (n t)").bitcast(I32),
+            )
+            planes = const.tile([P, PASSES, N], U8, name=label + "_planes", align_bytes=64)
+            nc.vector.memset(planes[:].bitcast(I32), 0)
+            for quad in range(QUADRANTS):
+                nc.sync.dma_start(
+                    out=planes[32 * quad : 32 * quad + 4].bitcast(I32),
+                    in_=scales[:, 4 * quad : 4 * quad + 4, :].rearrange("g r n -> r g n").bitcast(I32),
+                )
+            return codes, planes
+
+        def load_by_chunk(vector, label):
+            by_chunk = const.tile([P, PASSES, PACK], BF16, name=label)
+            nc.scalar.dma_start(out=by_chunk[:], in_=vector.rearrange("(g p t) -> p g t", g=PASSES, t=PACK))
+            return by_chunk[:].rearrange("p g t -> p (g t)")
+
+        def load_on_all_partitions(vector, label):
+            rows = const.tile([P, N], BF16, name=label)
+            nc.scalar.dma_start(out=rows[:], in_=vector.partition_broadcast(P))
+            return rows
+
+        c_z = const.tile([P, D], BF16, name="c_z")
+        nc.sync.dma_start(out=c_z[:], in_=c_z2)
+        c_gain = load_by_chunk(c_g2, "c_gain")
+        c_shift = load_by_chunk(c_be2, "c_shift")
+        c_codes, c_planes = load_weight(c_w3_words, c_w3_scales, "c_w")
+        s_gain = load_by_chunk(s_g2, "s_gain")
+        s_shift = load_by_chunk(s_be2, "s_shift")
+        s_codes, s_planes = load_weight(s_w3_words, s_w3_scales, "s_w")
+        c_bias = load_on_all_partitions(c_b3, "c_bias")
+        s_bias = load_on_all_partitions(s_b3, "s_bias")
+
+        units = [dict(rows=[c_z[:]], gain=c_gain, shift=c_shift, codes=c_codes, planes=c_planes)]
+        for first in range(0, S, LOAD_SLICES):
+            z_in = z_pool.tile([P, LOAD_SLICES, D], BF16, name="z_in")
+            nc.sync.dma_start(out=z_in[:], in_=s_z2[:, first : first + LOAD_SLICES, :])
+            for s in range(0, LOAD_SLICES, UNIT):
+                units.append(
+                    dict(
+                        rows=[z_in[:, s + i, :] for i in range(UNIT)],
+                        gain=s_gain,
+                        shift=s_shift,
+                        codes=s_codes,
+                        planes=s_planes,
+                    )
+                )
+
+        ident = const.tile([P, P], BF16, name="ident")
+        make_identity(nc, ident[:])
+        eps = const.tile([P, 1], F32, name="eps")
+        nc.vector.memset(eps[:], EPS)
+        gate = const.tile([P, N], F32, name="gate")
+        gated_bias = const.tile([P, N], F32, name="gated_bias")
+        best = const.tile([P, UNIT, N], F32, name="best")
+
+        def transpose(unit):
+            unit["banks"] = []
+            for z in unit["rows"]:
+                zt = zt_pool.tile([P, CHUNKS, B], BF16, name="zt")
+                by_byte = z.rearrange("b (g p t) -> b g t p", g=PASSES, t=PACK)
+                for g in range(PASSES):
+                    for t in range(PACK):
+                        nc.tensor.transpose(zt[:, g * PACK + t, :], by_byte[:, g, t, :], ident[:])
+                unit["banks"].append(zt)
+
+        def statistics(unit):
+            stats = small.tile([P, UNIT, CHUNKS, 3], F32, name="stats")
+            for s, zt in enumerate(unit["banks"]):
+                for j in range(0, CHUNKS, 2):
+                    nc.vector.bn_stats(
+                        out=stats[:, s, j : j + 2, :].rearrange("p e v -> p (e v)"),
+                        in_=zt[:, j : j + 2, :].rearrange("p e b -> p b e"),
+                    )
+            unit["stats"] = stats
+
+        def slope_and_offset(unit):
+            n = len(unit["banks"])
+            mean = unit["stats"][:, :n, :, 1]
+            count_var = unit["stats"][:, :n, :, 2]
+            every_slice = [P, n, CHUNKS]
+            std = small.tile([P, UNIT, CHUNKS], F32, name="std")
+            rstd = small.tile([P, UNIT, CHUNKS], F32, name="rstd")
+            slope = small.tile([P, UNIT, CHUNKS], F32, name="slope")
+            offset = small.tile([P, UNIT, CHUNKS], F32, name="offset")
+            nc.scalar.activation(out=std[:, :n], in_=count_var, func=FUNC.Sqrt, bias=eps[:], scale=1.0 / B)
+            nc.vector.reciprocal(out=rstd[:, :n], in_=std[:, :n])
+            nc.vector.tensor_tensor(
+                out=slope[:, :n], in0=rstd[:, :n], in1=unit["gain"].unsqueeze(1).to_broadcast(every_slice), op=ALU.mult
+            )
+            nc.vector.tensor_tensor(out=offset[:, :n], in0=slope[:, :n], in1=mean, op=ALU.mult)
+            nc.vector.tensor_tensor(
+                out=offset[:, :n],
+                in0=unit["shift"].unsqueeze(1).to_broadcast(every_slice),
+                in1=offset[:, :n],
+                op=ALU.subtract,
+            )
+            unit["slope"] = slope
+            unit["offset"] = offset
+
+        def normalise(unit):
+            h = work_pool.tile([P, UNIT, CHUNKS, B], BF16, name="h")
+            for s, zt in enumerate(unit["banks"]):
+                for j in range(CHUNKS):
+                    nc.scalar.activation(
+                        out=h[:, s, j, :],
+                        in_=zt[:, j, :],
+                        func=FUNC.Relu,
+                        bias=unit["offset"][:, s, j : j + 1],
+                        scale=unit["slope"][:, s, j : j + 1],
+                    )
+            unit["h"] = h
+
+        def regroup(unit):
+            grouped = work_pool.tile([P, UNIT, PASSES, B, PACK], BF16, name="grouped", align_bytes=64)
+            for s in range(len(unit["banks"])):
+                for g in range(PASSES):
+                    chunks = unit["h"][:, s, g * PACK : (g + 1) * PACK, :].rearrange("p t b -> p b t")
+                    if s * PASSES + g == VECTOR_PIECE:
+                        nc.vector.tensor_copy(out=grouped[:, s, g], in_=chunks)
+                    else:
+                        nc.scalar.copy(out=grouped[:, s, g], in_=chunks)
+            unit["grouped"] = grouped
+
+        def quantise(unit):
+            n = len(unit["banks"])
+            words = n * PASSES * B
+            h_codes = work_pool.tile([P, UNIT * PASSES * B], U32, name="h_codes", align_bytes=64)
+            h_planes = work_pool.tile([P, UNIT * PASSES * B], U8, name="h_planes", align_bytes=64)
+            nc.vector.quantize_mx(
+                out=h_codes[:, :words].bitcast(FP8X4),
+                scales=h_planes[:, :words],
+                in_=unit["grouped"][:, :n].rearrange("p s g b t -> p (s g b t)"),
+            )
+            unit["h_codes"] = h_codes
+            unit["h_planes"] = h_planes
+
+        def multiply(unit):
+            acc = acc_pool.tile([P, UNIT, N], F32, name="acc")
+            for s in range(len(unit["banks"])):
+                for g in range(PASSES):
+                    cols = slice((s * PASSES + g) * B, (s * PASSES + g + 1) * B)
+                    nc.tensor.matmul_mx(
+                        out=acc[:, s, :],
+                        lhsT=unit["h_codes"][:, cols].bitcast(FP8X4),
+                        lhsT_scale=unit["h_planes"][:, cols],
+                        rhs=unit["codes"][:, g, :].bitcast(FP8X4),
+                        rhs_scale=unit["planes"][:, g, :],
+                        start=(g == 0),
+                        stop=(g == PASSES - 1),
+                    )
+            unit["acc"] = acc
+
+        def make_gate(unit):
+            nc.vector.tensor_tensor(out=gate[:], in0=unit["acc"][:, 0, :], in1=c_bias[:], op=ALU.add)
+            nc.vector.tensor_tensor(out=gated_bias[:], in0=gate[:], in1=s_bias[:], op=ALU.mult)
+
+        def gate_and_store(unit, first_slice):
+            every_slice = [P, UNIT, N]
+            gated = out_pool.tile(every_slice, F32, name="gated")
+            nc.vector.tensor_tensor(
+                out=gated[:], in0=unit["acc"][:], in1=gate[:].unsqueeze(1).to_broadcast(every_slice), op=ALU.mult
+            )
+            nc.vector.tensor_tensor(
+                out=gated[:], in0=gated[:], in1=gated_bias[:].unsqueeze(1).to_broadcast(every_slice), op=ALU.add
+            )
+            if first_slice == 0:
+                nc.vector.tensor_copy(out=best[:], in_=gated[:])
+            else:
+                nc.vector.tensor_tensor(out=best[:], in0=best[:], in1=gated[:], op=ALU.max)
+            nc.sync.dma_start(out=out_0[:, first_slice : first_slice + UNIT, :], in_=gated[:])
+
+        def exists(u):
+            return 0 <= u < len(units)
+
+        for k in range(-1, len(units) + 2):
+            if exists(k + 1):
+                transpose(units[k + 1])
+            if exists(k - 1):
+                normalise(units[k - 1])
+            if exists(k):
+                slope_and_offset(units[k])
+            if exists(k - 1):
+                regroup(units[k - 1])
+            if k - 2 == 0:
+                make_gate(units[0])
+            elif exists(k - 2):
+                gate_and_store(units[k - 2], (k - 3) * UNIT)
+            if exists(k - 1):
+                quantise(units[k - 1])
+                multiply(units[k - 1])
+            if exists(k + 1):
+                statistics(units[k + 1])
+
+        pooled = const.tile([P, N], F32, name="pooled")
+        nc.vector.tensor_tensor(out=pooled[:], in0=best[:, 0, :], in1=best[:, 1, :], op=ALU.max)
+        nc.sync.dma_start(out=out_1, in_=pooled[:])

@@ -52,6 +52,7 @@ def tile_cgblock_pb_t_kernel(
         out_pool = ctx.enter_context(tc.tile_pool(name="out", bufs=3))
         zt_pool = ctx.enter_context(tc.psum_pool(name="zt", bufs=3 * UNIT))
         acc_pool = ctx.enter_context(tc.psum_pool(name="acc", bufs=2))
+        ctx.enter_context(tc.manual_schedule())
 
         def load_weight(words, scales, label):
             codes = const.tile([P, PASSES, N], U32, name=label + "_codes", align_bytes=64)

@@ -21,7 +21,8 @@ CHUNKS = PASSES * PACK
 UNIT = 2
 LOAD_SLICES = 4
 QUADRANTS = 4
-VECTOR_PIECE = 3
+VECTOR_PASS = 1
+RUN = 4
 
 FLOPS = 2 * (B * S + B) * D * N
 
@@ -52,7 +53,6 @@ def tile_cgblock_pb_t_kernel(
         out_pool = ctx.enter_context(tc.tile_pool(name="out", bufs=3))
         zt_pool = ctx.enter_context(tc.psum_pool(name="zt", bufs=3 * UNIT))
         acc_pool = ctx.enter_context(tc.psum_pool(name="acc", bufs=2))
-        ctx.enter_context(tc.manual_schedule())
 
         def load_weight(words, scales, label):
             codes = const.tile([P, PASSES, N], U32, name=label + "_codes", align_bytes=64)
@@ -144,11 +144,11 @@ def tile_cgblock_pb_t_kernel(
             offset = small.tile([P, UNIT, CHUNKS], F32, name="offset")
             nc.scalar.activation(out=std[:, :n], in_=count_var, func=FUNC.Sqrt, bias=eps[:], scale=1.0 / B)
             nc.vector.reciprocal(out=rstd[:, :n], in_=std[:, :n])
-            nc.vector.tensor_tensor(
+            nc.gpsimd.tensor_tensor(
                 out=slope[:, :n], in0=rstd[:, :n], in1=unit["gain"].unsqueeze(1).to_broadcast(every_slice), op=ALU.mult
             )
-            nc.vector.tensor_tensor(out=offset[:, :n], in0=slope[:, :n], in1=mean, op=ALU.mult)
-            nc.vector.tensor_tensor(
+            nc.gpsimd.tensor_tensor(out=offset[:, :n], in0=slope[:, :n], in1=mean, op=ALU.mult)
+            nc.gpsimd.tensor_tensor(
                 out=offset[:, :n],
                 in0=unit["shift"].unsqueeze(1).to_broadcast(every_slice),
                 in1=offset[:, :n],
@@ -174,11 +174,12 @@ def tile_cgblock_pb_t_kernel(
             grouped = work_pool.tile([P, UNIT, PASSES, B, PACK], BF16, name="grouped", align_bytes=64)
             for s in range(len(unit["banks"])):
                 for g in range(PASSES):
-                    chunks = unit["h"][:, s, g * PACK : (g + 1) * PACK, :].rearrange("p t b -> p b t")
-                    if s * PASSES + g == VECTOR_PIECE:
-                        nc.vector.tensor_copy(out=grouped[:, s, g], in_=chunks)
+                    chunks = unit["h"][:, s, g * PACK : (g + 1) * PACK, :].rearrange("p t (c i) -> p c t i", i=RUN)
+                    words = grouped[:, s, g].rearrange("p (c i) t -> p c t i", i=RUN)
+                    if g == VECTOR_PASS:
+                        nc.vector.tensor_copy(out=words, in_=chunks)
                     else:
-                        nc.scalar.copy(out=grouped[:, s, g], in_=chunks)
+                        nc.scalar.copy(out=words, in_=chunks)
             unit["grouped"] = grouped
 
         def quantise(unit):
@@ -216,17 +217,18 @@ def tile_cgblock_pb_t_kernel(
 
         def gate_and_store(unit, first_slice):
             every_slice = [P, UNIT, N]
+            product = out_pool.tile(every_slice, F32, name="product")
             gated = out_pool.tile(every_slice, F32, name="gated")
             nc.vector.tensor_tensor(
-                out=gated[:], in0=unit["acc"][:], in1=gate[:].unsqueeze(1).to_broadcast(every_slice), op=ALU.mult
+                out=product[:], in0=unit["acc"][:], in1=gate[:].unsqueeze(1).to_broadcast(every_slice), op=ALU.mult
             )
-            nc.vector.tensor_tensor(
-                out=gated[:], in0=gated[:], in1=gated_bias[:].unsqueeze(1).to_broadcast(every_slice), op=ALU.add
+            nc.gpsimd.tensor_tensor(
+                out=gated[:], in0=product[:], in1=gated_bias[:].unsqueeze(1).to_broadcast(every_slice), op=ALU.add
             )
             if first_slice == 0:
-                nc.vector.tensor_copy(out=best[:], in_=gated[:])
+                nc.vector.tensor_copy(out=best[:], in_=product[:])
             else:
-                nc.vector.tensor_tensor(out=best[:], in0=best[:], in1=gated[:], op=ALU.max)
+                nc.vector.tensor_tensor(out=best[:], in0=best[:], in1=product[:], op=ALU.max)
             nc.sync.dma_start(out=out_0[:, first_slice : first_slice + UNIT, :], in_=gated[:])
 
         def exists(u):
@@ -253,4 +255,5 @@ def tile_cgblock_pb_t_kernel(
 
         pooled = const.tile([P, N], F32, name="pooled")
         nc.vector.tensor_tensor(out=pooled[:], in0=best[:, 0, :], in1=best[:, 1, :], op=ALU.max)
+        nc.vector.tensor_tensor(out=pooled[:], in0=pooled[:], in1=gated_bias[:], op=ALU.add)
         nc.sync.dma_start(out=out_1, in_=pooled[:])

@@ -21,7 +21,6 @@ CHUNKS = PASSES * PACK
 UNIT = 2
 LOAD_SLICES = 4
 QUADRANTS = 4
-VECTOR_PASS = 1
 RUN = 4
 
 FLOPS = 2 * (B * S + B) * D * N
@@ -53,6 +52,7 @@ def tile_cgblock_pb_t_kernel(
         out_pool = ctx.enter_context(tc.tile_pool(name="out", bufs=3))
         zt_pool = ctx.enter_context(tc.psum_pool(name="zt", bufs=3 * UNIT))
         acc_pool = ctx.enter_context(tc.psum_pool(name="acc", bufs=2))
+        ctx.enter_context(tc.manual_schedule())
 
         def load_weight(words, scales, label):
             codes = const.tile([P, PASSES, N], U32, name=label + "_codes", align_bytes=64)
@@ -90,7 +90,7 @@ def tile_cgblock_pb_t_kernel(
         c_bias = load_on_all_partitions(c_b3, "c_bias")
         s_bias = load_on_all_partitions(s_b3, "s_bias")
 
-        units = [dict(rows=[c_z[:]], gain=c_gain, shift=c_shift, codes=c_codes, planes=c_planes)]
+        units = [dict(rows=[c_z[:]], gain=c_gain, shift=c_shift, codes=c_codes, planes=c_planes, first_slice=None)]
         for first in range(0, S, LOAD_SLICES):
             z_in = z_pool.tile([P, LOAD_SLICES, D], BF16, name="z_in")
             nc.sync.dma_start(out=z_in[:], in_=s_z2[:, first : first + LOAD_SLICES, :])
@@ -102,6 +102,7 @@ def tile_cgblock_pb_t_kernel(
                         shift=s_shift,
                         codes=s_codes,
                         planes=s_planes,
+                        first_slice=first + s,
                     )
                 )
 
@@ -122,65 +123,80 @@ def tile_cgblock_pb_t_kernel(
                     for t in range(PACK):
                         nc.tensor.transpose(zt[:, g * PACK + t, :], by_byte[:, g, t, :], ident[:])
                 unit["banks"].append(zt)
-
-        def statistics(unit):
             stats = small.tile([P, UNIT, CHUNKS, 3], F32, name="stats")
-            for s, zt in enumerate(unit["banks"]):
-                for j in range(0, CHUNKS, 2):
-                    nc.vector.bn_stats(
-                        out=stats[:, s, j : j + 2, :].rearrange("p e v -> p (e v)"),
-                        in_=zt[:, j : j + 2, :].rearrange("p e b -> p b e"),
-                    )
             unit["stats"] = stats
 
-        def slope_and_offset(unit):
-            n = len(unit["banks"])
-            mean = unit["stats"][:, :n, :, 1]
-            count_var = unit["stats"][:, :n, :, 2]
-            every_slice = [P, n, CHUNKS]
-            std = small.tile([P, UNIT, CHUNKS], F32, name="std")
-            rstd = small.tile([P, UNIT, CHUNKS], F32, name="rstd")
-            slope = small.tile([P, UNIT, CHUNKS], F32, name="slope")
-            offset = small.tile([P, UNIT, CHUNKS], F32, name="offset")
-            nc.scalar.activation(out=std[:, :n], in_=count_var, func=FUNC.Sqrt, bias=eps[:], scale=1.0 / B)
-            nc.vector.reciprocal(out=rstd[:, :n], in_=std[:, :n])
-            nc.gpsimd.tensor_tensor(
-                out=slope[:, :n], in0=rstd[:, :n], in1=unit["gain"].unsqueeze(1).to_broadcast(every_slice), op=ALU.mult
+        def statistics(unit, s, j):
+            nc.vector.bn_stats(
+                out=unit["stats"][:, s, j : j + 2, :].rearrange("p e v -> p (e v)"),
+                in_=unit["banks"][s][:, j : j + 2, :].rearrange("p e b -> p b e"),
             )
-            nc.gpsimd.tensor_tensor(out=offset[:, :n], in0=slope[:, :n], in1=mean, op=ALU.mult)
-            nc.gpsimd.tensor_tensor(
-                out=offset[:, :n],
-                in0=unit["shift"].unsqueeze(1).to_broadcast(every_slice),
-                in1=offset[:, :n],
+
+        def deviation(unit):
+            n = len(unit["banks"])
+            std = small.tile([P, UNIT, CHUNKS], F32, name="std")
+            nc.scalar.activation(
+                out=std[:, :n], in_=unit["stats"][:, :n, :, 2], func=FUNC.Sqrt, bias=eps[:], scale=1.0 / B
+            )
+            unit["std"] = std
+
+        def inverse_deviation(unit):
+            n = len(unit["banks"])
+            rstd = small.tile([P, UNIT, CHUNKS], F32, name="rstd")
+            nc.vector.reciprocal(out=rstd[:, :n], in_=unit["std"][:, :n])
+            unit["rstd"] = rstd
+
+        def slope(unit):
+            n = len(unit["banks"])
+            slopes = small.tile([P, UNIT, CHUNKS], F32, name="slopes")
+            nc.vector.tensor_tensor(
+                out=slopes[:, :n],
+                in0=unit["rstd"][:, :n],
+                in1=unit["gain"].unsqueeze(1).to_broadcast([P, n, CHUNKS]),
+                op=ALU.mult,
+            )
+            unit["slopes"] = slopes
+
+        def slope_times_mean(unit):
+            n = len(unit["banks"])
+            scaled_mean = small.tile([P, UNIT, CHUNKS], F32, name="scaled_mean")
+            nc.vector.tensor_tensor(
+                out=scaled_mean[:, :n], in0=unit["slopes"][:, :n], in1=unit["stats"][:, :n, :, 1], op=ALU.mult
+            )
+            unit["scaled_mean"] = scaled_mean
+
+        def offset(unit):
+            n = len(unit["banks"])
+            offsets = small.tile([P, UNIT, CHUNKS], F32, name="offsets")
+            nc.vector.tensor_tensor(
+                out=offsets[:, :n],
+                in0=unit["shift"].unsqueeze(1).to_broadcast([P, n, CHUNKS]),
+                in1=unit["scaled_mean"][:, :n],
                 op=ALU.subtract,
             )
-            unit["slope"] = slope
-            unit["offset"] = offset
+            unit["offsets"] = offsets
 
-        def normalise(unit):
-            h = work_pool.tile([P, UNIT, CHUNKS, B], BF16, name="h")
-            for s, zt in enumerate(unit["banks"]):
-                for j in range(CHUNKS):
-                    nc.scalar.activation(
-                        out=h[:, s, j, :],
-                        in_=zt[:, j, :],
-                        func=FUNC.Relu,
-                        bias=unit["offset"][:, s, j : j + 1],
-                        scale=unit["slope"][:, s, j : j + 1],
-                    )
-            unit["h"] = h
+        def normalise(unit, s):
+            if s == 0:
+                h = work_pool.tile([P, UNIT, CHUNKS, B], BF16, name="h")
+                unit["h"] = h
+            for j in range(CHUNKS):
+                nc.scalar.activation(
+                    out=unit["h"][:, s, j, :],
+                    in_=unit["banks"][s][:, j, :],
+                    func=FUNC.Relu,
+                    bias=unit["offsets"][:, s, j : j + 1],
+                    scale=unit["slopes"][:, s, j : j + 1],
+                )
 
-        def regroup(unit):
-            grouped = work_pool.tile([P, UNIT, PASSES, B, PACK], BF16, name="grouped", align_bytes=64)
-            for s in range(len(unit["banks"])):
-                for g in range(PASSES):
-                    chunks = unit["h"][:, s, g * PACK : (g + 1) * PACK, :].rearrange("p t (c i) -> p c t i", i=RUN)
-                    words = grouped[:, s, g].rearrange("p (c i) t -> p c t i", i=RUN)
-                    if g == VECTOR_PASS:
-                        nc.vector.tensor_copy(out=words, in_=chunks)
-                    else:
-                        nc.scalar.copy(out=words, in_=chunks)
-            unit["grouped"] = grouped
+        def regroup(unit, s, g, copy):
+            if (s, g) == (0, 0):
+                grouped = work_pool.tile([P, UNIT, PASSES, B, PACK], BF16, name="grouped", align_bytes=64)
+                unit["grouped"] = grouped
+            copy(
+                out=unit["grouped"][:, s, g].rearrange("p (c i) t -> p c t i", i=RUN),
+                in_=unit["h"][:, s, g * PACK : (g + 1) * PACK, :].rearrange("p t (c i) -> p c t i", i=RUN),
+            )
 
         def quantise(unit):
             n = len(unit["banks"])
@@ -211,49 +227,68 @@ def tile_cgblock_pb_t_kernel(
                     )
             unit["acc"] = acc
 
-        def make_gate(unit):
-            nc.vector.tensor_tensor(out=gate[:], in0=unit["acc"][:, 0, :], in1=c_bias[:], op=ALU.add)
-            nc.vector.tensor_tensor(out=gated_bias[:], in0=gate[:], in1=s_bias[:], op=ALU.mult)
+        every_slice = [P, UNIT, N]
 
-        def gate_and_store(unit, first_slice):
-            every_slice = [P, UNIT, N]
-            product = out_pool.tile(every_slice, F32, name="product")
-            gated = out_pool.tile(every_slice, F32, name="gated")
-            nc.vector.tensor_tensor(
-                out=product[:], in0=unit["acc"][:], in1=gate[:].unsqueeze(1).to_broadcast(every_slice), op=ALU.mult
-            )
-            nc.gpsimd.tensor_tensor(
-                out=gated[:], in0=product[:], in1=gated_bias[:].unsqueeze(1).to_broadcast(every_slice), op=ALU.add
-            )
-            if first_slice == 0:
-                nc.vector.tensor_copy(out=best[:], in_=product[:])
+        def finish_first(unit):
+            if unit["first_slice"] is None:
+                nc.vector.tensor_tensor(out=gate[:], in0=unit["acc"][:, 0, :], in1=c_bias[:], op=ALU.add)
             else:
-                nc.vector.tensor_tensor(out=best[:], in0=best[:], in1=product[:], op=ALU.max)
-            nc.sync.dma_start(out=out_0[:, first_slice : first_slice + UNIT, :], in_=gated[:])
+                gated = out_pool.tile(every_slice, F32, name="gated")
+                nc.vector.tensor_tensor(
+                    out=gated[:], in0=unit["acc"][:], in1=gate[:].unsqueeze(1).to_broadcast(every_slice), op=ALU.mult
+                )
+                unit["gated"] = gated
 
-        def exists(u):
-            return 0 <= u < len(units)
+        def finish_second(unit):
+            if unit["first_slice"] is None:
+                nc.vector.tensor_tensor(out=gated_bias[:], in0=gate[:], in1=s_bias[:], op=ALU.mult)
+            else:
+                nc.vector.tensor_tensor(
+                    out=unit["gated"][:],
+                    in0=unit["gated"][:],
+                    in1=gated_bias[:].unsqueeze(1).to_broadcast(every_slice),
+                    op=ALU.add,
+                )
 
-        for k in range(-1, len(units) + 2):
-            if exists(k + 1):
-                transpose(units[k + 1])
-            if exists(k - 1):
-                normalise(units[k - 1])
-            if exists(k):
-                slope_and_offset(units[k])
-            if exists(k - 1):
-                regroup(units[k - 1])
-            if k - 2 == 0:
-                make_gate(units[0])
-            elif exists(k - 2):
-                gate_and_store(units[k - 2], (k - 3) * UNIT)
-            if exists(k - 1):
-                quantise(units[k - 1])
-                multiply(units[k - 1])
-            if exists(k + 1):
-                statistics(units[k + 1])
+        def finish_third(unit):
+            first_slice = unit["first_slice"]
+            if first_slice is None:
+                return
+            if first_slice == 0:
+                nc.vector.tensor_copy(out=best[:], in_=unit["gated"][:])
+            else:
+                nc.vector.tensor_tensor(out=best[:], in0=best[:], in1=unit["gated"][:], op=ALU.max)
+            nc.sync.dma_start(out=out_0[:, first_slice : first_slice + UNIT, :], in_=unit["gated"][:])
+
+        def do(stage, u, *where):
+            if 0 <= u < len(units) and (len(where) == 0 or where[0] < len(units[u]["rows"])):
+                stage(units[u], *where)
+
+        for k in range(-1, len(units) + 3):
+            do(transpose, k + 1)
+            for j in range(0, CHUNKS, 2):
+                do(statistics, k, 1, j)
+            do(quantise, k - 2)
+            do(multiply, k - 2)
+            do(normalise, k - 1, 0)
+            do(deviation, k)
+            do(normalise, k - 1, 1)
+            do(finish_first, k - 3)
+            do(inverse_deviation, k)
+            do(statistics, k + 1, 0, 0)
+            do(finish_second, k - 3)
+            do(slope, k)
+            do(statistics, k + 1, 0, 2)
+            do(finish_third, k - 3)
+            do(slope_times_mean, k)
+            do(regroup, k - 1, 0, 0, nc.scalar.copy)
+            do(regroup, k - 1, 0, 1, nc.scalar.copy)
+            do(regroup, k - 1, 1, 0, nc.scalar.copy)
+            do(regroup, k - 1, 1, 1, nc.vector.tensor_copy)
+            do(offset, k)
+            do(statistics, k + 1, 0, 4)
+            do(statistics, k + 1, 0, 6)
 
         pooled = const.tile([P, N], F32, name="pooled")
         nc.vector.tensor_tensor(out=pooled[:], in0=best[:, 0, :], in1=best[:, 1, :], op=ALU.max)
-        nc.vector.tensor_tensor(out=pooled[:], in0=pooled[:], in1=gated_bias[:], op=ALU.add)
         nc.sync.dma_start(out=out_1, in_=pooled[:])

@@ -240,15 +240,18 @@ def tile_cgblock_pb_t_kernel(
                 unit["gated"] = gated
 
         def finish_second(unit):
-            if unit["first_slice"] is None:
+            first_slice = unit["first_slice"]
+            if first_slice is None:
                 nc.vector.tensor_tensor(out=gated_bias[:], in0=gate[:], in1=s_bias[:], op=ALU.mult)
             else:
-                nc.vector.tensor_tensor(
-                    out=unit["gated"][:],
+                result = out_pool.tile(every_slice, F32, name="result")
+                nc.gpsimd.tensor_tensor(
+                    out=result[:],
                     in0=unit["gated"][:],
                     in1=gated_bias[:].unsqueeze(1).to_broadcast(every_slice),
                     op=ALU.add,
                 )
+                nc.sync.dma_start(out=out_0[:, first_slice : first_slice + UNIT, :], in_=result[:])
 
         def finish_third(unit):
             first_slice = unit["first_slice"]
@@ -258,7 +261,6 @@ def tile_cgblock_pb_t_kernel(
                 nc.vector.tensor_copy(out=best[:], in_=unit["gated"][:])
             else:
                 nc.vector.tensor_tensor(out=best[:], in0=best[:], in1=unit["gated"][:], op=ALU.max)
-            nc.sync.dma_start(out=out_0[:, first_slice : first_slice + UNIT, :], in_=unit["gated"][:])
 
         def do(stage, u, *where):
             if 0 <= u < len(units) and (len(where) == 0 or where[0] < len(units[u]["rows"])):
@@ -266,29 +268,30 @@ def tile_cgblock_pb_t_kernel(
 
         for k in range(-1, len(units) + 3):
             do(transpose, k + 1)
+            do(finish_first, k - 3)
+            do(finish_second, k - 3)
             for j in range(0, CHUNKS, 2):
                 do(statistics, k, 1, j)
+            do(statistics, k + 1, 0, 0)
             do(quantise, k - 2)
             do(multiply, k - 2)
             do(normalise, k - 1, 0)
             do(deviation, k)
             do(normalise, k - 1, 1)
-            do(finish_first, k - 3)
             do(inverse_deviation, k)
-            do(statistics, k + 1, 0, 0)
-            do(finish_second, k - 3)
+            do(finish_third, k - 3)
             do(slope, k)
             do(statistics, k + 1, 0, 2)
-            do(finish_third, k - 3)
+            do(statistics, k + 1, 0, 4)
             do(slope_times_mean, k)
             do(regroup, k - 1, 0, 0, nc.scalar.copy)
             do(regroup, k - 1, 0, 1, nc.scalar.copy)
             do(regroup, k - 1, 1, 0, nc.scalar.copy)
             do(regroup, k - 1, 1, 1, nc.vector.tensor_copy)
             do(offset, k)
-            do(statistics, k + 1, 0, 4)
             do(statistics, k + 1, 0, 6)
 
         pooled = const.tile([P, N], F32, name="pooled")
         nc.vector.tensor_tensor(out=pooled[:], in0=best[:, 0, :], in1=best[:, 1, :], op=ALU.max)
+        nc.vector.tensor_tensor(out=pooled[:], in0=pooled[:], in1=gated_bias[:], op=ALU.add)
         nc.sync.dma_start(out=out_1, in_=pooled[:])

@@ -83,17 +83,23 @@ def tile_cgblock_pb_t_kernel(
         nc.sync.dma_start(out=c_z[:], in_=c_z2)
         c_gain = load_by_chunk(c_g2, "c_gain")
         c_shift = load_by_chunk(c_be2, "c_shift")
-        c_codes, c_planes = load_weight(c_w3_words, c_w3_scales, "c_w")
         s_gain = load_by_chunk(s_g2, "s_gain")
         s_shift = load_by_chunk(s_be2, "s_shift")
-        s_codes, s_planes = load_weight(s_w3_words, s_w3_scales, "s_w")
         c_bias = load_on_all_partitions(c_b3, "c_bias")
         s_bias = load_on_all_partitions(s_b3, "s_bias")
 
-        units = [dict(rows=[c_z[:]], gain=c_gain, shift=c_shift, codes=c_codes, planes=c_planes, first_slice=None)]
+        units = [dict(rows=[c_z[:]], gain=c_gain, shift=c_shift, first_slice=None)]
         for first in range(0, S, LOAD_SLICES):
             z_in = z_pool.tile([P, LOAD_SLICES, D], BF16, name="z_in")
-            nc.sync.dma_start(out=z_in[:], in_=s_z2[:, first : first + LOAD_SLICES, :])
+            if first == 0:
+                for s in range(0, LOAD_SLICES, UNIT):
+                    nc.sync.dma_start(out=z_in[:, s : s + UNIT, :], in_=s_z2[:, s : s + UNIT, :])
+                c_codes, c_planes = load_weight(c_w3_words, c_w3_scales, "c_w")
+                s_codes, s_planes = load_weight(s_w3_words, s_w3_scales, "s_w")
+                units[0]["codes"] = c_codes
+                units[0]["planes"] = c_planes
+            else:
+                nc.sync.dma_start(out=z_in[:], in_=s_z2[:, first : first + LOAD_SLICES, :])
             for s in range(0, LOAD_SLICES, UNIT):
                 units.append(
                     dict(
@@ -110,6 +116,8 @@ def tile_cgblock_pb_t_kernel(
         make_identity(nc, ident[:])
         eps = const.tile([P, 1], F32, name="eps")
         nc.vector.memset(eps[:], EPS)
+        warm = const.tile([P, 1], F32, name="warm")
+        nc.scalar.activation(out=warm[:], in_=eps[:], func=FUNC.Sqrt)
         gate = const.tile([P, N], F32, name="gate")
         gated_bias = const.tile([P, N], F32, name="gated_bias")
         best = const.tile([P, UNIT, N], F32, name="best")
@@ -239,13 +247,13 @@ def tile_cgblock_pb_t_kernel(
                 )
                 unit["gated"] = gated
 
-        def finish_second(unit):
+        def finish_second(unit, engine):
             first_slice = unit["first_slice"]
             if first_slice is None:
                 nc.vector.tensor_tensor(out=gated_bias[:], in0=gate[:], in1=s_bias[:], op=ALU.mult)
             else:
                 result = out_pool.tile(every_slice, F32, name="result")
-                nc.gpsimd.tensor_tensor(
+                engine.tensor_tensor(
                     out=result[:],
                     in0=unit["gated"][:],
                     in1=gated_bias[:].unsqueeze(1).to_broadcast(every_slice),
@@ -269,7 +277,8 @@ def tile_cgblock_pb_t_kernel(
         for k in range(-1, len(units) + 3):
             do(transpose, k + 1)
             do(finish_first, k - 3)
-            do(finish_second, k - 3)
+            adder = nc.gpsimd if k < len(units) else nc.vector
+            do(lambda unit: finish_second(unit, adder), k - 3)
             for j in range(0, CHUNKS, 2):
                 do(statistics, k, 1, j)
             do(statistics, k + 1, 0, 0)

@@ -279,9 +279,9 @@ def tile_cgblock_pb_t_kernel(
             do(finish_first, k - 3)
             adder = nc.gpsimd if k < len(units) else nc.vector
             do(lambda unit: finish_second(unit, adder), k - 3)
-            for j in range(0, CHUNKS, 2):
+            for j in range(CHUNKS - 2, -1, -2):
                 do(statistics, k, 1, j)
-            do(statistics, k + 1, 0, 0)
+            do(statistics, k + 1, 0, 6)
             do(quantise, k - 2)
             do(multiply, k - 2)
             do(normalise, k - 1, 0)
@@ -290,15 +290,15 @@ def tile_cgblock_pb_t_kernel(
             do(inverse_deviation, k)
             do(finish_third, k - 3)
             do(slope, k)
-            do(statistics, k + 1, 0, 2)
             do(statistics, k + 1, 0, 4)
+            do(statistics, k + 1, 0, 2)
             do(slope_times_mean, k)
             do(regroup, k - 1, 0, 0, nc.scalar.copy)
             do(regroup, k - 1, 0, 1, nc.scalar.copy)
             do(regroup, k - 1, 1, 0, nc.scalar.copy)
             do(regroup, k - 1, 1, 1, nc.vector.tensor_copy)
             do(offset, k)
-            do(statistics, k + 1, 0, 6)
+            do(statistics, k + 1, 0, 0)
 
         pooled = const.tile([P, N], F32, name="pooled")
         nc.vector.tensor_tensor(out=pooled[:], in0=best[:, 0, :], in1=best[:, 1, :], op=ALU.max)

@@ -49,6 +49,7 @@ def tile_cgblock_pb_t_kernel(
         z_pool = ctx.enter_context(tc.tile_pool(name="z", bufs=S // LOAD_SLICES))
         small = ctx.enter_context(tc.tile_pool(name="small", bufs=3))
         work_pool = ctx.enter_context(tc.tile_pool(name="work", bufs=2))
+        port_pool = ctx.enter_context(tc.tile_pool(name="port", bufs=1))
         out_pool = ctx.enter_context(tc.tile_pool(name="out", bufs=3))
         zt_pool = ctx.enter_context(tc.psum_pool(name="zt", bufs=3 * UNIT))
         acc_pool = ctx.enter_context(tc.psum_pool(name="acc", bufs=2))
@@ -184,11 +185,11 @@ def tile_cgblock_pb_t_kernel(
             )
             unit["offsets"] = offsets
 
-        def normalise(unit, s):
-            if s == 0:
+        def normalise(unit, s, chunks=range(CHUNKS)):
+            if (s, chunks[0]) == (0, 0):
                 h = work_pool.tile([P, UNIT, CHUNKS, B], BF16, name="h")
                 unit["h"] = h
-            for j in range(CHUNKS):
+            for j in chunks:
                 nc.scalar.activation(
                     out=unit["h"][:, s, j, :],
                     in_=unit["banks"][s][:, j, :],
@@ -197,43 +198,54 @@ def tile_cgblock_pb_t_kernel(
                     scale=unit["slopes"][:, s, j : j + 1],
                 )
 
-        def regroup(unit, s, g, copy):
-            if (s, g) == (0, 0):
-                grouped = work_pool.tile([P, UNIT, PASSES, B, PACK], BF16, name="grouped", align_bytes=64)
-                unit["grouped"] = grouped
-            copy(
-                out=unit["grouped"][:, s, g].rearrange("p (c i) t -> p c t i", i=RUN),
+        def regroup_on_scalar(unit, s, g):
+            if g == 0:
+                grouped = work_pool.tile([P, PASSES, B, PACK], BF16, name="grouped", align_bytes=64)
+                unit["grouped"] = [grouped]
+            nc.scalar.copy(
+                out=unit["grouped"][s][:, g].rearrange("p (c i) t -> p c t i", i=RUN),
                 in_=unit["h"][:, s, g * PACK : (g + 1) * PACK, :].rearrange("p t (c i) -> p c t i", i=RUN),
             )
 
-        def quantise(unit):
-            n = len(unit["banks"])
-            words = n * PASSES * B
-            h_codes = work_pool.tile([P, UNIT * PASSES * B], U32, name="h_codes", align_bytes=64)
-            h_planes = work_pool.tile([P, UNIT * PASSES * B], U8, name="h_planes", align_bytes=64)
-            nc.vector.quantize_mx(
-                out=h_codes[:, :words].bitcast(FP8X4),
-                scales=h_planes[:, :words],
-                in_=unit["grouped"][:, :n].rearrange("p s g b t -> p (s g b t)"),
-            )
-            unit["h_codes"] = h_codes
-            unit["h_planes"] = h_planes
+        def regroup_second(unit, s, engine):
+            second = port_pool.tile([P, PASSES, B, PACK], BF16, name="second", align_bytes=64)
+            unit["grouped"].append(second)
+            for g in range(PASSES):
+                engine.tensor_scalar(
+                    out=second[:, g],
+                    in0=unit["h"][:, s, g * PACK : (g + 1) * PACK, :].rearrange("p t b -> p b t"),
+                    scalar1=1.0,
+                    scalar2=0.0,
+                    op0=ALU.mult,
+                    op1=ALU.add,
+                )
 
-        def multiply(unit):
-            acc = acc_pool.tile([P, UNIT, N], F32, name="acc")
-            for s in range(len(unit["banks"])):
-                for g in range(PASSES):
-                    cols = slice((s * PASSES + g) * B, (s * PASSES + g + 1) * B)
-                    nc.tensor.matmul_mx(
-                        out=acc[:, s, :],
-                        lhsT=unit["h_codes"][:, cols].bitcast(FP8X4),
-                        lhsT_scale=unit["h_planes"][:, cols],
-                        rhs=unit["codes"][:, g, :].bitcast(FP8X4),
-                        rhs_scale=unit["planes"][:, g, :],
-                        start=(g == 0),
-                        stop=(g == PASSES - 1),
-                    )
-            unit["acc"] = acc
+        def quantise(unit, s):
+            if s == 0:
+                h_codes = work_pool.tile([P, UNIT, PASSES, B], U32, name="h_codes", align_bytes=64)
+                h_planes = work_pool.tile([P, UNIT, PASSES, B], U8, name="h_planes", align_bytes=64)
+                unit["h_codes"] = h_codes
+                unit["h_planes"] = h_planes
+            nc.vector.quantize_mx(
+                out=unit["h_codes"][:, s].rearrange("p g b -> p (g b)").bitcast(FP8X4),
+                scales=unit["h_planes"][:, s].rearrange("p g b -> p (g b)"),
+                in_=unit["grouped"][s][:].rearrange("p g b t -> p (g b t)"),
+            )
+
+        def multiply(unit, s):
+            if s == 0:
+                acc = acc_pool.tile([P, UNIT, N], F32, name="acc")
+                unit["acc"] = acc
+            for g in range(PASSES):
+                nc.tensor.matmul_mx(
+                    out=unit["acc"][:, s, :],
+                    lhsT=unit["h_codes"][:, s, g, :].bitcast(FP8X4),
+                    lhsT_scale=unit["h_planes"][:, s, g, :],
+                    rhs=unit["codes"][:, g, :].bitcast(FP8X4),
+                    rhs_scale=unit["planes"][:, g, :],
+                    start=(g == 0),
+                    stop=(g == PASSES - 1),
+                )
 
         every_slice = [P, UNIT, N]
 
@@ -261,44 +273,49 @@ def tile_cgblock_pb_t_kernel(
                 )
                 nc.sync.dma_start(out=out_0[:, first_slice : first_slice + UNIT, :], in_=result[:])
 
-        def finish_third(unit):
+        def finish_third(unit, s):
             first_slice = unit["first_slice"]
             if first_slice is None:
                 return
             if first_slice == 0:
-                nc.vector.tensor_copy(out=best[:], in_=unit["gated"][:])
+                nc.vector.tensor_copy(out=best[:, s, :], in_=unit["gated"][:, s, :])
             else:
-                nc.vector.tensor_tensor(out=best[:], in0=best[:], in1=unit["gated"][:], op=ALU.max)
+                nc.vector.tensor_tensor(out=best[:, s, :], in0=best[:, s, :], in1=unit["gated"][:, s, :], op=ALU.max)
 
         def do(stage, u, *where):
             if 0 <= u < len(units) and (len(where) == 0 or where[0] < len(units[u]["rows"])):
                 stage(units[u], *where)
 
-        for k in range(-1, len(units) + 3):
+        last = len(units) - 1
+        for k in range(-1, last + 4):
             do(transpose, k + 1)
+            for j in range(0, CHUNKS, 2):
+                do(statistics, k, 0, j)
             do(finish_first, k - 3)
-            adder = nc.gpsimd if k < len(units) else nc.vector
-            do(lambda unit: finish_second(unit, adder), k - 3)
-            for j in range(CHUNKS - 2, -1, -2):
+            for j in range(0, CHUNKS, 2):
                 do(statistics, k, 1, j)
-            do(statistics, k + 1, 0, 6)
-            do(quantise, k - 2)
-            do(multiply, k - 2)
+            if k - 2 < last:
+                do(regroup_second, k - 2, 1, nc.gpsimd)
+            adder = nc.gpsimd if k <= last else nc.vector
+            do(lambda unit: finish_second(unit, adder), k - 3)
             do(normalise, k - 1, 0)
+            do(regroup_on_scalar, k - 1, 0, 0)
+            do(regroup_on_scalar, k - 1, 0, 1)
+            do(normalise, k - 1, 1, range(2))
             do(deviation, k)
-            do(normalise, k - 1, 1)
+            do(normalise, k - 1, 1, range(2, CHUNKS))
+            do(finish_third, k - 3, 0)
             do(inverse_deviation, k)
-            do(finish_third, k - 3)
+            do(finish_third, k - 3, 1)
             do(slope, k)
-            do(statistics, k + 1, 0, 4)
-            do(statistics, k + 1, 0, 2)
+            do(quantise, k - 2, 0)
+            do(multiply, k - 2, 0)
             do(slope_times_mean, k)
-            do(regroup, k - 1, 0, 0, nc.scalar.copy)
-            do(regroup, k - 1, 0, 1, nc.scalar.copy)
-            do(regroup, k - 1, 1, 0, nc.scalar.copy)
-            do(regroup, k - 1, 1, 1, nc.vector.tensor_copy)
+            do(quantise, k - 2, 1)
+            do(multiply, k - 2, 1)
             do(offset, k)
-            do(statistics, k + 1, 0, 0)
+            if k - 1 == last:
+                do(regroup_second, k - 1, 1, nc.vector)
 
         pooled = const.tile([P, N], F32, name="pooled")
         nc.vector.tensor_tensor(out=pooled[:], in0=best[:, 0, :], in1=best[:, 1, :], op=ALU.max)

@@ -21,6 +21,7 @@ CHUNKS = PASSES * PACK
 UNIT = 2
 LOAD_SLICES = 4
 QUADRANTS = 4
+GPSIMD_ROWS = 96
 RUN = 4
 
 FLOPS = 2 * (B * S + B) * D * N
@@ -51,6 +52,7 @@ def tile_cgblock_pb_t_kernel(
         work_pool = ctx.enter_context(tc.tile_pool(name="work", bufs=2))
         port_pool = ctx.enter_context(tc.tile_pool(name="port", bufs=1))
         out_pool = ctx.enter_context(tc.tile_pool(name="out", bufs=3))
+        result_pool = ctx.enter_context(tc.tile_pool(name="results", bufs=8))
         zt_pool = ctx.enter_context(tc.psum_pool(name="zt", bufs=3 * UNIT))
         acc_pool = ctx.enter_context(tc.psum_pool(name="acc", bufs=2))
         ctx.enter_context(tc.manual_schedule())
@@ -207,17 +209,48 @@ def tile_cgblock_pb_t_kernel(
                 in_=unit["h"][:, s, g * PACK : (g + 1) * PACK, :].rearrange("p t (c i) -> p c t i", i=RUN),
             )
 
-        def regroup_second(unit, s, engine):
+        def regroup_on_gpsimd(unit, s):
+            second = port_pool.tile([P, PASSES, B, PACK], BF16, name="second", align_bytes=64)
+            unit["grouped"].append(second)
+            nc.gpsimd.tensor_scalar(
+                out=second[:, :, :GPSIMD_ROWS, :],
+                in0=unit["h"][:, s, :, :GPSIMD_ROWS].rearrange("p (g t) b -> p g b t", t=PACK),
+                scalar1=1.0,
+                scalar2=0.0,
+                op0=ALU.mult,
+                op1=ALU.add,
+            )
+
+        def regroup_rest(unit, s):
+            for g in range(PASSES):
+                nc.scalar.copy(
+                    out=unit["grouped"][s][:, g, GPSIMD_ROWS:].rearrange("p (c i) t -> p c t i", i=RUN),
+                    in_=unit["h"][:, s, g * PACK : (g + 1) * PACK, GPSIMD_ROWS:].rearrange(
+                        "p t (c i) -> p c t i", i=RUN
+                    ),
+                )
+
+        def normalise_on_vector(unit, s):
+            for j in range(CHUNKS):
+                nc.vector.tensor_scalar(
+                    out=unit["h"][:, s, j, :],
+                    in0=unit["banks"][s][:, j, :],
+                    scalar1=unit["slopes"][:, s, j : j + 1],
+                    scalar2=unit["offsets"][:, s, j : j + 1],
+                    op0=ALU.mult,
+                    op1=ALU.add,
+                )
+
+        def regroup_on_vector(unit, s):
             second = port_pool.tile([P, PASSES, B, PACK], BF16, name="second", align_bytes=64)
             unit["grouped"].append(second)
             for g in range(PASSES):
-                engine.tensor_scalar(
-                    out=second[:, g],
-                    in0=unit["h"][:, s, g * PACK : (g + 1) * PACK, :].rearrange("p t b -> p b t"),
-                    scalar1=1.0,
-                    scalar2=0.0,
-                    op0=ALU.mult,
-                    op1=ALU.add,
+                nc.vector.tensor_scalar(
+                    out=second[:, g].rearrange("p (c i) t -> p c t i", i=RUN),
+                    in0=unit["h"][:, s, g * PACK : (g + 1) * PACK, :].rearrange("p t (c i) -> p c t i", i=RUN),
+                    scalar1=0.0,
+                    scalar2=None,
+                    op0=ALU.max,
                 )
 
         def quantise(unit, s):
@@ -264,7 +297,7 @@ def tile_cgblock_pb_t_kernel(
             if first_slice is None:
                 nc.vector.tensor_tensor(out=gated_bias[:], in0=gate[:], in1=s_bias[:], op=ALU.mult)
             else:
-                result = out_pool.tile(every_slice, F32, name="result")
+                result = result_pool.tile(every_slice, F32, name="result")
                 engine.tensor_tensor(
                     out=result[:],
                     in0=unit["gated"][:],
@@ -287,23 +320,22 @@ def tile_cgblock_pb_t_kernel(
                 stage(units[u], *where)
 
         last = len(units) - 1
-        for k in range(-1, last + 4):
+        for k in range(-1, last + 1):
             do(transpose, k + 1)
             for j in range(0, CHUNKS, 2):
-                do(statistics, k, 0, j)
+                do(statistics, k, 1, j)
             do(finish_first, k - 3)
             for j in range(0, CHUNKS, 2):
-                do(statistics, k, 1, j)
-            if k - 2 < last:
-                do(regroup_second, k - 2, 1, nc.gpsimd)
-            adder = nc.gpsimd if k <= last else nc.vector
-            do(lambda unit: finish_second(unit, adder), k - 3)
+                do(statistics, k + 1, 0, j)
+            if k - 2 > 0:
+                do(regroup_on_gpsimd, k - 2, 1)
+            do(lambda unit: finish_second(unit, nc.gpsimd), k - 3)
+            do(regroup_rest, k - 2, 1)
             do(normalise, k - 1, 0)
             do(regroup_on_scalar, k - 1, 0, 0)
-            do(regroup_on_scalar, k - 1, 0, 1)
-            do(normalise, k - 1, 1, range(2))
             do(deviation, k)
-            do(normalise, k - 1, 1, range(2, CHUNKS))
+            do(regroup_on_scalar, k - 1, 0, 1)
+            do(normalise, k - 1, 1)
             do(finish_third, k - 3, 0)
             do(inverse_deviation, k)
             do(finish_third, k - 3, 1)
@@ -314,8 +346,35 @@ def tile_cgblock_pb_t_kernel(
             do(quantise, k - 2, 1)
             do(multiply, k - 2, 1)
             do(offset, k)
-            if k - 1 == last:
-                do(regroup_second, k - 1, 1, nc.vector)
+
+        before, previous, final = units[-3:]
+        regroup_on_gpsimd(previous, 1)
+        regroup_rest(previous, 1)
+        normalise(final, 0)
+        regroup_on_scalar(final, 0, 0)
+        regroup_on_scalar(final, 0, 1)
+        normalise_on_vector(final, 1)
+        finish_first(before)
+        quantise(previous, 0)
+        multiply(previous, 0)
+        quantise(previous, 1)
+        multiply(previous, 1)
+        finish_second(before, nc.vector)
+        regroup_on_vector(final, 1)
+        finish_first(previous)
+        quantise(final, 0)
+        multiply(final, 0)
+        quantise(final, 1)
+        multiply(final, 1)
+        finish_third(before, 0)
+        finish_third(before, 1)
+        finish_second(previous, nc.vector)
+        finish_third(previous, 0)
+        finish_first(final)
+        finish_third(previous, 1)
+        finish_second(final, nc.vector)
+        finish_third(final, 0)
+        finish_third(final, 1)
 
         pooled = const.tile([P, N], F32, name="pooled")
         nc.vector.tensor_tensor(out=pooled[:], in0=best[:, 0, :], in1=best[:, 1, :], op=ALU.max)

@@ -21,8 +21,8 @@ CHUNKS = PASSES * PACK
 UNIT = 2
 LOAD_SLICES = 4
 QUADRANTS = 4
-GPSIMD_ROWS = 96
-RUN = 4
+GPSIMD_ROWS = 112
+RUN = 8
 
 FLOPS = 2 * (B * S + B) * D * N
 
@@ -125,17 +125,17 @@ def tile_cgblock_pb_t_kernel(
         gated_bias = const.tile([P, N], F32, name="gated_bias")
         best = const.tile([P, UNIT, N], F32, name="best")
 
-        def transpose(unit):
-            unit["banks"] = []
-            for z in unit["rows"]:
-                zt = zt_pool.tile([P, CHUNKS, B], BF16, name="zt")
-                by_byte = z.rearrange("b (g p t) -> b g t p", g=PASSES, t=PACK)
-                for g in range(PASSES):
-                    for t in range(PACK):
-                        nc.tensor.transpose(zt[:, g * PACK + t, :], by_byte[:, g, t, :], ident[:])
-                unit["banks"].append(zt)
-            stats = small.tile([P, UNIT, CHUNKS, 3], F32, name="stats")
-            unit["stats"] = stats
+        def transpose(unit, s):
+            if s == 0:
+                unit["banks"] = []
+                stats = small.tile([P, UNIT, CHUNKS, 3], F32, name="stats")
+                unit["stats"] = stats
+            zt = zt_pool.tile([P, CHUNKS, B], BF16, name="zt")
+            by_byte = unit["rows"][s].rearrange("b (g p t) -> b g t p", g=PASSES, t=PACK)
+            for g in range(PASSES):
+                for t in range(PACK):
+                    nc.tensor.transpose(zt[:, g * PACK + t, :], by_byte[:, g, t, :], ident[:])
+            unit["banks"].append(zt)
 
         def statistics(unit, s, j):
             nc.vector.bn_stats(
@@ -144,7 +144,7 @@ def tile_cgblock_pb_t_kernel(
             )
 
         def deviation(unit):
-            n = len(unit["banks"])
+            n = len(unit["rows"])
             std = small.tile([P, UNIT, CHUNKS], F32, name="std")
             nc.scalar.activation(
                 out=std[:, :n], in_=unit["stats"][:, :n, :, 2], func=FUNC.Sqrt, bias=eps[:], scale=1.0 / B
@@ -152,13 +152,13 @@ def tile_cgblock_pb_t_kernel(
             unit["std"] = std
 
         def inverse_deviation(unit):
-            n = len(unit["banks"])
+            n = len(unit["rows"])
             rstd = small.tile([P, UNIT, CHUNKS], F32, name="rstd")
             nc.vector.reciprocal(out=rstd[:, :n], in_=unit["std"][:, :n])
             unit["rstd"] = rstd
 
         def slope(unit):
-            n = len(unit["banks"])
+            n = len(unit["rows"])
             slopes = small.tile([P, UNIT, CHUNKS], F32, name="slopes")
             nc.vector.tensor_tensor(
                 out=slopes[:, :n],
@@ -169,7 +169,7 @@ def tile_cgblock_pb_t_kernel(
             unit["slopes"] = slopes
 
         def slope_times_mean(unit):
-            n = len(unit["banks"])
+            n = len(unit["rows"])
             scaled_mean = small.tile([P, UNIT, CHUNKS], F32, name="scaled_mean")
             nc.vector.tensor_tensor(
                 out=scaled_mean[:, :n], in0=unit["slopes"][:, :n], in1=unit["stats"][:, :n, :, 1], op=ALU.mult
@@ -177,7 +177,7 @@ def tile_cgblock_pb_t_kernel(
             unit["scaled_mean"] = scaled_mean
 
         def offset(unit):
-            n = len(unit["banks"])
+            n = len(unit["rows"])
             offsets = small.tile([P, UNIT, CHUNKS], F32, name="offsets")
             nc.vector.tensor_tensor(
                 out=offsets[:, :n],
@@ -200,11 +200,11 @@ def tile_cgblock_pb_t_kernel(
                     scale=unit["slopes"][:, s, j : j + 1],
                 )
 
-        def regroup_on_scalar(unit, s, g):
+        def regroup_first(unit, s, g, copy):
             if g == 0:
                 grouped = work_pool.tile([P, PASSES, B, PACK], BF16, name="grouped", align_bytes=64)
                 unit["grouped"] = [grouped]
-            nc.scalar.copy(
+            copy(
                 out=unit["grouped"][s][:, g].rearrange("p (c i) t -> p c t i", i=RUN),
                 in_=unit["h"][:, s, g * PACK : (g + 1) * PACK, :].rearrange("p t (c i) -> p c t i", i=RUN),
             )
@@ -241,16 +241,14 @@ def tile_cgblock_pb_t_kernel(
                     op1=ALU.add,
                 )
 
-        def regroup_on_vector(unit, s):
+        def regroup_with_relu(unit, s):
             second = port_pool.tile([P, PASSES, B, PACK], BF16, name="second", align_bytes=64)
             unit["grouped"].append(second)
             for g in range(PASSES):
-                nc.vector.tensor_scalar(
+                nc.scalar.activation(
                     out=second[:, g].rearrange("p (c i) t -> p c t i", i=RUN),
-                    in0=unit["h"][:, s, g * PACK : (g + 1) * PACK, :].rearrange("p t (c i) -> p c t i", i=RUN),
-                    scalar1=0.0,
-                    scalar2=None,
-                    op0=ALU.max,
+                    in_=unit["h"][:, s, g * PACK : (g + 1) * PACK, :].rearrange("p t (c i) -> p c t i", i=RUN),
+                    func=FUNC.Relu,
                 )
 
         def quantise(unit, s):
@@ -306,39 +304,40 @@ def tile_cgblock_pb_t_kernel(
                 )
                 nc.sync.dma_start(out=out_0[:, first_slice : first_slice + UNIT, :], in_=result[:])
 
-        def finish_third(unit, s):
+        def finish_third(unit):
             first_slice = unit["first_slice"]
             if first_slice is None:
                 return
             if first_slice == 0:
-                nc.vector.tensor_copy(out=best[:, s, :], in_=unit["gated"][:, s, :])
+                nc.vector.tensor_copy(out=best[:], in_=unit["gated"][:])
             else:
-                nc.vector.tensor_tensor(out=best[:, s, :], in0=best[:, s, :], in1=unit["gated"][:, s, :], op=ALU.max)
+                nc.vector.tensor_tensor(out=best[:], in0=best[:], in1=unit["gated"][:], op=ALU.max)
 
         def do(stage, u, *where):
             if 0 <= u < len(units) and (len(where) == 0 or where[0] < len(units[u]["rows"])):
                 stage(units[u], *where)
 
         last = len(units) - 1
+        do(transpose, 0, 0)
         for k in range(-1, last + 1):
-            do(transpose, k + 1)
+            do(transpose, k + 1, 1)
+            do(finish_first, k - 4)
             for j in range(0, CHUNKS, 2):
                 do(statistics, k, 1, j)
-            do(finish_first, k - 3)
             for j in range(0, CHUNKS, 2):
                 do(statistics, k + 1, 0, j)
             if k - 2 > 0:
                 do(regroup_on_gpsimd, k - 2, 1)
-            do(lambda unit: finish_second(unit, nc.gpsimd), k - 3)
-            do(regroup_rest, k - 2, 1)
+            do(lambda unit: finish_second(unit, nc.gpsimd), k - 4)
             do(normalise, k - 1, 0)
-            do(regroup_on_scalar, k - 1, 0, 0)
+            do(transpose, k + 2, 0)
             do(deviation, k)
-            do(regroup_on_scalar, k - 1, 0, 1)
+            do(regroup_rest, k - 2, 1)
             do(normalise, k - 1, 1)
-            do(finish_third, k - 3, 0)
+            do(regroup_first, k - 1, 0, 0, nc.scalar.copy)
+            do(regroup_first, k - 1, 0, 1, nc.scalar.copy)
             do(inverse_deviation, k)
-            do(finish_third, k - 3, 1)
+            do(finish_third, k - 4)
             do(slope, k)
             do(quantise, k - 2, 0)
             do(multiply, k - 2, 0)
@@ -347,34 +346,34 @@ def tile_cgblock_pb_t_kernel(
             do(multiply, k - 2, 1)
             do(offset, k)
 
-        before, previous, final = units[-3:]
+        first, before, previous, final = units[-4:]
         regroup_on_gpsimd(previous, 1)
         regroup_rest(previous, 1)
         normalise(final, 0)
-        regroup_on_scalar(final, 0, 0)
-        regroup_on_scalar(final, 0, 1)
+        regroup_first(final, 0, 0, nc.scalar.copy)
+        regroup_first(final, 0, 1, nc.scalar.copy)
+        finish_first(first)
         normalise_on_vector(final, 1)
+        finish_second(first, nc.gpsimd)
         finish_first(before)
         quantise(previous, 0)
         multiply(previous, 0)
+        finish_third(first)
         quantise(previous, 1)
         multiply(previous, 1)
+        regroup_with_relu(final, 1)
         finish_second(before, nc.vector)
-        regroup_on_vector(final, 1)
-        finish_first(previous)
+        finish_third(before)
         quantise(final, 0)
         multiply(final, 0)
+        finish_first(previous)
         quantise(final, 1)
         multiply(final, 1)
-        finish_third(before, 0)
-        finish_third(before, 1)
         finish_second(previous, nc.vector)
-        finish_third(previous, 0)
+        finish_third(previous)
         finish_first(final)
-        finish_third(previous, 1)
         finish_second(final, nc.vector)
-        finish_third(final, 0)
-        finish_third(final, 1)
+        finish_third(final)
 
         pooled = const.tile([P, N], F32, name="pooled")
         nc.vector.tensor_tensor(out=pooled[:], in0=best[:, 0, :], in1=best[:, 1, :], op=ALU.max)

@@ -21,7 +21,7 @@ CHUNKS = PASSES * PACK
 UNIT = 2
 LOAD_SLICES = 4
 QUADRANTS = 4
-GPSIMD_ROWS = 112
+GPSIMD_ROWS = 64
 RUN = 8
 
 FLOPS = 2 * (B * S + B) * D * N
@@ -290,6 +290,22 @@ def tile_cgblock_pb_t_kernel(
                 )
                 unit["gated"] = gated
 
+        def finish_last(unit):
+            pooled = const.tile([P, UNIT, N], F32, name="pooled")
+            result = result_pool.tile(every_slice, F32, name="result")
+            nc.vector.tensor_tensor(out=pooled[:, 0], in0=best[:, 0, :], in1=best[:, 1, :], op=ALU.max)
+            finish_first(unit)
+            for s in range(UNIT):
+                nc.vector.tensor_tensor(
+                    out=result[:, s, :], in0=unit["gated"][:, s, :], in1=gated_bias[:], op=ALU.add
+                )
+                nc.sync.dma_start(out=out_0[:, unit["first_slice"] + s, :], in_=result[:, s, :])
+                nc.vector.tensor_tensor(
+                    out=pooled[:, 1 - s], in0=pooled[:, s], in1=unit["gated"][:, s, :], op=ALU.max
+                )
+            nc.vector.tensor_tensor(out=pooled[:, 1], in0=pooled[:, 0], in1=gated_bias[:], op=ALU.add)
+            nc.sync.dma_start(out=out_1, in_=pooled[:, 1])
+
         def finish_second(unit, engine):
             first_slice = unit["first_slice"]
             if first_slice is None:
@@ -324,8 +340,11 @@ def tile_cgblock_pb_t_kernel(
             do(finish_first, k - 4)
             for j in range(0, CHUNKS, 2):
                 do(statistics, k, 1, j)
-            for j in range(0, CHUNKS, 2):
-                do(statistics, k + 1, 0, j)
+            if k == last:
+                do(finish_first, k - 3)
+            if k > 2:
+                for j in range(0, CHUNKS, 2):
+                    do(statistics, k + 1, 0, j)
             if k - 2 > 0:
                 do(regroup_on_gpsimd, k - 2, 1)
             do(lambda unit: finish_second(unit, nc.gpsimd), k - 4)
@@ -336,6 +355,20 @@ def tile_cgblock_pb_t_kernel(
             do(normalise, k - 1, 1)
             do(regroup_first, k - 1, 0, 0, nc.scalar.copy)
             do(regroup_first, k - 1, 0, 1, nc.scalar.copy)
+            if k <= 2:
+                do(statistics, k + 1, 0, 0)
+                do(inverse_deviation, k)
+                do(statistics, k + 1, 0, 2)
+                do(slope, k)
+                do(statistics, k + 1, 0, 4)
+                do(quantise, k - 2, 0)
+                do(multiply, k - 2, 0)
+                do(slope_times_mean, k)
+                do(statistics, k + 1, 0, 6)
+                do(quantise, k - 2, 1)
+                do(multiply, k - 2, 1)
+                do(offset, k)
+                continue
             do(inverse_deviation, k)
             do(finish_third, k - 4)
             do(slope, k)
@@ -352,30 +385,22 @@ def tile_cgblock_pb_t_kernel(
         normalise(final, 0)
         regroup_first(final, 0, 0, nc.scalar.copy)
         regroup_first(final, 0, 1, nc.scalar.copy)
-        finish_first(first)
         normalise_on_vector(final, 1)
-        finish_second(first, nc.gpsimd)
         finish_first(before)
         quantise(previous, 0)
         multiply(previous, 0)
-        finish_third(first)
         quantise(previous, 1)
         multiply(previous, 1)
+        finish_second(first, nc.vector)
+        finish_third(first)
         regroup_with_relu(final, 1)
         finish_second(before, nc.vector)
         finish_third(before)
+        finish_first(previous)
         quantise(final, 0)
         multiply(final, 0)
-        finish_first(previous)
         quantise(final, 1)
         multiply(final, 1)
         finish_second(previous, nc.vector)
         finish_third(previous)
-        finish_first(final)
-        finish_second(final, nc.vector)
-        finish_third(final)
-
-        pooled = const.tile([P, N], F32, name="pooled")
-        nc.vector.tensor_tensor(out=pooled[:], in0=best[:, 0, :], in1=best[:, 1, :], op=ALU.max)
-        nc.vector.tensor_tensor(out=pooled[:], in0=pooled[:], in1=gated_bias[:], op=ALU.add)
-        nc.sync.dma_start(out=out_1, in_=pooled[:])
+        finish_last(final)

@@ -21,7 +21,7 @@ CHUNKS = PASSES * PACK
 UNIT = 2
 LOAD_SLICES = 4
 QUADRANTS = 4
-GPSIMD_ROWS = 64
+GPSIMD_ROWS = 112
 RUN = 8
 
 FLOPS = 2 * (B * S + B) * D * N
@@ -53,8 +53,9 @@ def tile_cgblock_pb_t_kernel(
         port_pool = ctx.enter_context(tc.tile_pool(name="port", bufs=1))
         out_pool = ctx.enter_context(tc.tile_pool(name="out", bufs=3))
         result_pool = ctx.enter_context(tc.tile_pool(name="results", bufs=8))
-        zt_pool = ctx.enter_context(tc.psum_pool(name="zt", bufs=3 * UNIT))
-        acc_pool = ctx.enter_context(tc.psum_pool(name="acc", bufs=2))
+        zt_pool = ctx.enter_context(tc.psum_pool(name="zt", bufs=6))
+        mean_pool = ctx.enter_context(tc.psum_pool(name="mean", bufs=1))
+        acc_pool = ctx.enter_context(tc.psum_pool(name="acc", bufs=1))
         ctx.enter_context(tc.manual_schedule())
 
         def load_weight(words, scales, label):
@@ -91,7 +92,7 @@ def tile_cgblock_pb_t_kernel(
         c_bias = load_on_all_partitions(c_b3, "c_bias")
         s_bias = load_on_all_partitions(s_b3, "s_bias")
 
-        units = [dict(rows=[c_z[:]], gain=c_gain, shift=c_shift, first_slice=None)]
+        units = [dict(rows=[c_z[:]], gain=c_gain, shift=c_shift, first_slice=None, squares=False)]
         for first in range(0, S, LOAD_SLICES):
             z_in = z_pool.tile([P, LOAD_SLICES, D], BF16, name="z_in")
             if first == 0:
@@ -112,11 +113,15 @@ def tile_cgblock_pb_t_kernel(
                         codes=s_codes,
                         planes=s_planes,
                         first_slice=first + s,
+                        parity=len(units) % 2,
+                        squares=len(units) > 4 and len(units) % 3 > 0,
                     )
                 )
 
         ident = const.tile([P, P], BF16, name="ident")
         make_identity(nc, ident[:])
+        mean_column = const.tile([P, 1], BF16, name="mean_column")
+        nc.vector.memset(mean_column[:], 1.0 / B)
         eps = const.tile([P, 1], F32, name="eps")
         nc.vector.memset(eps[:], EPS)
         warm = const.tile([P, 1], F32, name="warm")
@@ -124,6 +129,8 @@ def tile_cgblock_pb_t_kernel(
         gate = const.tile([P, N], F32, name="gate")
         gated_bias = const.tile([P, N], F32, name="gated_bias")
         best = const.tile([P, UNIT, N], F32, name="best")
+
+        means = mean_pool.tile([P, 2, 2], F32, name="means")
 
         def transpose(unit, s):
             if s == 0:
@@ -135,9 +142,37 @@ def tile_cgblock_pb_t_kernel(
             for g in range(PASSES):
                 for t in range(PACK):
                     nc.tensor.transpose(zt[:, g * PACK + t, :], by_byte[:, g, t, :], ident[:])
+            if s == 0 and unit["squares"]:
+                for i in range(2):
+                    nc.tensor.matmul(
+                        means[:, unit["parity"], i : i + 1],
+                        lhsT=by_byte[:, 1, 2 + i, :],
+                        rhs=mean_column[:],
+                        start=True,
+                        stop=True,
+                    )
             unit["banks"].append(zt)
 
+        def fetch_means(unit, s):
+            if unit["squares"]:
+                nc.scalar.copy(out=unit["stats"][:, s, 6:8, 1], in_=means[:, unit["parity"], :])
+
+        def square(unit, s):
+            if unit["squares"]:
+                junk = work_pool.tile([P, 2, B], BF16, name="junk")
+                for i in range(2):
+                    nc.scalar.activation(
+                        out=junk[:, i, :],
+                        in_=unit["banks"][s][:, 6 + i, :],
+                        func=FUNC.Square,
+                        bias=unit["stats"][:, s, 6 + i, 1:2],
+                        scale=-1.0,
+                        accum_out=unit["stats"][:, s, 6 + i, 2:3],
+                    )
+
         def statistics(unit, s, j):
+            if s == 0 and j == 6 and unit["squares"]:
+                return
             nc.vector.bn_stats(
                 out=unit["stats"][:, s, j : j + 2, :].rearrange("p e v -> p (e v)"),
                 in_=unit["banks"][s][:, j : j + 2, :].rearrange("p e b -> p b e"),
@@ -337,17 +372,21 @@ def tile_cgblock_pb_t_kernel(
         do(transpose, 0, 0)
         for k in range(-1, last + 1):
             do(transpose, k + 1, 1)
-            do(finish_first, k - 4)
-            for j in range(0, CHUNKS, 2):
-                do(statistics, k, 1, j)
-            if k == last:
-                do(finish_first, k - 3)
-            if k > 2:
-                for j in range(0, CHUNKS, 2):
-                    do(statistics, k + 1, 0, j)
+            reads = [(k, 1, j) for j in range(0, CHUNKS, 2)] + [(k + 1, 0, j) for j in range(0, CHUNKS, 2)]
+            if k <= 2:
+                reads = reads[: CHUNKS // 2]
+            for read in reads[:8]:
+                do(statistics, *read)
+            do(finish_first, k - 3)
+            for read in reads[8:]:
+                do(statistics, *read)
             if k - 2 > 0:
                 do(regroup_on_gpsimd, k - 2, 1)
             do(lambda unit: finish_second(unit, nc.gpsimd), k - 4)
+            if k <= 2:
+                do(statistics, k + 1, 0, 0)
+                do(statistics, k + 1, 0, 2)
+            do(fetch_means, k + 1, 0)
             do(normalise, k - 1, 0)
             do(transpose, k + 2, 0)
             do(deviation, k)
@@ -355,23 +394,14 @@ def tile_cgblock_pb_t_kernel(
             do(normalise, k - 1, 1)
             do(regroup_first, k - 1, 0, 0, nc.scalar.copy)
             do(regroup_first, k - 1, 0, 1, nc.scalar.copy)
-            if k <= 2:
-                do(statistics, k + 1, 0, 0)
-                do(inverse_deviation, k)
-                do(statistics, k + 1, 0, 2)
-                do(slope, k)
-                do(statistics, k + 1, 0, 4)
-                do(quantise, k - 2, 0)
-                do(multiply, k - 2, 0)
-                do(slope_times_mean, k)
-                do(statistics, k + 1, 0, 6)
-                do(quantise, k - 2, 1)
-                do(multiply, k - 2, 1)
-                do(offset, k)
-                continue
+            do(square, k + 1, 0)
             do(inverse_deviation, k)
+            if k <= 2:
+                do(statistics, k + 1, 0, 4)
             do(finish_third, k - 4)
             do(slope, k)
+            if k <= 2:
+                do(statistics, k + 1, 0, 6)
             do(quantise, k - 2, 0)
             do(multiply, k - 2, 0)
             do(slope_times_mean, k)

@@ -21,7 +21,7 @@ CHUNKS = PASSES * PACK
 UNIT = 2
 LOAD_SLICES = 4
 QUADRANTS = 4
-GPSIMD_ROWS = 112
+GPSIMD_ROWS = 208
 RUN = 8
 
 FLOPS = 2 * (B * S + B) * D * N
@@ -114,7 +114,7 @@ def tile_cgblock_pb_t_kernel(
                         planes=s_planes,
                         first_slice=first + s,
                         parity=len(units) % 2,
-                        squares=len(units) > 4 and len(units) % 3 > 0,
+                        squares=len(units) > 4 and len(units) % 2 == 1,
                     )
                 )
 
@@ -224,32 +224,34 @@ def tile_cgblock_pb_t_kernel(
 
         def normalise(unit, s, chunks=range(CHUNKS)):
             if (s, chunks[0]) == (0, 0):
-                h = work_pool.tile([P, UNIT, CHUNKS, B], BF16, name="h")
+                h = work_pool.tile([P, UNIT, PACK, PASSES, B], BF16, name="h")
                 unit["h"] = h
             for j in chunks:
                 nc.scalar.activation(
-                    out=unit["h"][:, s, j, :],
+                    out=unit["h"][:, s, j % PACK, j // PACK, :],
                     in_=unit["banks"][s][:, j, :],
                     func=FUNC.Relu,
                     bias=unit["offsets"][:, s, j : j + 1],
                     scale=unit["slopes"][:, s, j : j + 1],
                 )
 
-        def regroup_first(unit, s, g, copy):
-            if g == 0:
-                grouped = work_pool.tile([P, PASSES, B, PACK], BF16, name="grouped", align_bytes=64)
-                unit["grouped"] = [grouped]
-            copy(
-                out=unit["grouped"][s][:, g].rearrange("p (c i) t -> p c t i", i=RUN),
-                in_=unit["h"][:, s, g * PACK : (g + 1) * PACK, :].rearrange("p t (c i) -> p c t i", i=RUN),
-            )
+        def chunks_of(unit, s):
+            return unit["h"][:, s].rearrange("p t g b -> p t (g b)")
+
+        def copy_rows(copy, out, in_):
+            copy(out=out.rearrange("p (c i) t -> p c t i", i=RUN), in_=in_.rearrange("p t (c i) -> p c t i", i=RUN))
+
+        def regroup_first(unit, s):
+            grouped = work_pool.tile([P, PASSES * B, PACK], BF16, name="grouped", align_bytes=64)
+            unit["grouped"] = [grouped]
+            copy_rows(nc.scalar.copy, grouped[:], chunks_of(unit, s))
 
         def regroup_on_gpsimd(unit, s):
-            second = port_pool.tile([P, PASSES, B, PACK], BF16, name="second", align_bytes=64)
+            second = port_pool.tile([P, PASSES * B, PACK], BF16, name="second", align_bytes=64)
             unit["grouped"].append(second)
             nc.gpsimd.tensor_scalar(
-                out=second[:, :, :GPSIMD_ROWS, :],
-                in0=unit["h"][:, s, :, :GPSIMD_ROWS].rearrange("p (g t) b -> p g b t", t=PACK),
+                out=second[:, :GPSIMD_ROWS, :],
+                in0=chunks_of(unit, s)[:, :, :GPSIMD_ROWS].rearrange("p t r -> p r t"),
                 scalar1=1.0,
                 scalar2=0.0,
                 op0=ALU.mult,
@@ -257,18 +259,14 @@ def tile_cgblock_pb_t_kernel(
             )
 
         def regroup_rest(unit, s):
-            for g in range(PASSES):
-                nc.scalar.copy(
-                    out=unit["grouped"][s][:, g, GPSIMD_ROWS:].rearrange("p (c i) t -> p c t i", i=RUN),
-                    in_=unit["h"][:, s, g * PACK : (g + 1) * PACK, GPSIMD_ROWS:].rearrange(
-                        "p t (c i) -> p c t i", i=RUN
-                    ),
-                )
+            copy_rows(
+                nc.scalar.copy, unit["grouped"][s][:, GPSIMD_ROWS:, :], chunks_of(unit, s)[:, :, GPSIMD_ROWS:]
+            )
 
         def normalise_on_vector(unit, s):
             for j in range(CHUNKS):
                 nc.vector.tensor_scalar(
-                    out=unit["h"][:, s, j, :],
+                    out=unit["h"][:, s, j % PACK, j // PACK, :],
                     in0=unit["banks"][s][:, j, :],
                     scalar1=unit["slopes"][:, s, j : j + 1],
                     scalar2=unit["offsets"][:, s, j : j + 1],
@@ -276,18 +274,16 @@ def tile_cgblock_pb_t_kernel(
                     op1=ALU.add,
                 )
 
+        def relu_on_scalar(out, in_):
+            nc.scalar.activation(out=out, in_=in_, func=FUNC.Relu)
+
         def regroup_with_relu(unit, s):
-            second = port_pool.tile([P, PASSES, B, PACK], BF16, name="second", align_bytes=64)
+            second = port_pool.tile([P, PASSES * B, PACK], BF16, name="second", align_bytes=64)
             unit["grouped"].append(second)
-            for g in range(PASSES):
-                nc.scalar.activation(
-                    out=second[:, g].rearrange("p (c i) t -> p c t i", i=RUN),
-                    in_=unit["h"][:, s, g * PACK : (g + 1) * PACK, :].rearrange("p t (c i) -> p c t i", i=RUN),
-                    func=FUNC.Relu,
-                )
+            copy_rows(relu_on_scalar, second[:], chunks_of(unit, s))
 
         def quantise(unit, s):
-            if s == 0:
+            if "h_codes" not in unit:
                 h_codes = work_pool.tile([P, UNIT, PASSES, B], U32, name="h_codes", align_bytes=64)
                 h_planes = work_pool.tile([P, UNIT, PASSES, B], U8, name="h_planes", align_bytes=64)
                 unit["h_codes"] = h_codes
@@ -295,11 +291,11 @@ def tile_cgblock_pb_t_kernel(
             nc.vector.quantize_mx(
                 out=unit["h_codes"][:, s].rearrange("p g b -> p (g b)").bitcast(FP8X4),
                 scales=unit["h_planes"][:, s].rearrange("p g b -> p (g b)"),
-                in_=unit["grouped"][s][:].rearrange("p g b t -> p (g b t)"),
+                in_=unit["grouped"][s][:].rearrange("p r t -> p (r t)"),
             )
 
         def multiply(unit, s):
-            if s == 0:
+            if "acc" not in unit:
                 acc = acc_pool.tile([P, UNIT, N], F32, name="acc")
                 unit["acc"] = acc
             for g in range(PASSES):
@@ -375,10 +371,7 @@ def tile_cgblock_pb_t_kernel(
             reads = [(k, 1, j) for j in range(0, CHUNKS, 2)] + [(k + 1, 0, j) for j in range(0, CHUNKS, 2)]
             if k <= 2:
                 reads = reads[: CHUNKS // 2]
-            for read in reads[:8]:
-                do(statistics, *read)
-            do(finish_first, k - 3)
-            for read in reads[8:]:
+            for read in reads:
                 do(statistics, *read)
             if k - 2 > 0:
                 do(regroup_on_gpsimd, k - 2, 1)
@@ -392,29 +385,30 @@ def tile_cgblock_pb_t_kernel(
             do(deviation, k)
             do(regroup_rest, k - 2, 1)
             do(normalise, k - 1, 1)
-            do(regroup_first, k - 1, 0, 0, nc.scalar.copy)
-            do(regroup_first, k - 1, 0, 1, nc.scalar.copy)
+            do(regroup_first, k - 1, 0)
             do(square, k + 1, 0)
-            do(inverse_deviation, k)
+            if k > 2:
+                do(inverse_deviation, k)
+            do(finish_first, k - 3)
             if k <= 2:
+                do(inverse_deviation, k)
                 do(statistics, k + 1, 0, 4)
-            do(finish_third, k - 4)
             do(slope, k)
+            do(finish_third, k - 4)
             if k <= 2:
                 do(statistics, k + 1, 0, 6)
-            do(quantise, k - 2, 0)
-            do(multiply, k - 2, 0)
             do(slope_times_mean, k)
             do(quantise, k - 2, 1)
             do(multiply, k - 2, 1)
             do(offset, k)
+            do(quantise, k - 2, 0)
+            do(multiply, k - 2, 0)
 
         first, before, previous, final = units[-4:]
         regroup_on_gpsimd(previous, 1)
         regroup_rest(previous, 1)
         normalise(final, 0)
-        regroup_first(final, 0, 0, nc.scalar.copy)
-        regroup_first(final, 0, 1, nc.scalar.copy)
+        regroup_first(final, 0)
         normalise_on_vector(final, 1)
         finish_first(before)
         quantise(previous, 0)

@@ -21,7 +21,7 @@ CHUNKS = PASSES * PACK
 UNIT = 2
 LOAD_SLICES = 4
 QUADRANTS = 4
-GPSIMD_ROWS = 208
+GPSIMD_ROWS = 224
 RUN = 8
 
 FLOPS = 2 * (B * S + B) * D * N
@@ -92,31 +92,35 @@ def tile_cgblock_pb_t_kernel(
         c_bias = load_on_all_partitions(c_b3, "c_bias")
         s_bias = load_on_all_partitions(s_b3, "s_bias")
 
-        units = [dict(rows=[c_z[:]], gain=c_gain, shift=c_shift, first_slice=None, squares=False)]
+        loads = []
         for first in range(0, S, LOAD_SLICES):
-            z_in = z_pool.tile([P, LOAD_SLICES, D], BF16, name="z_in")
-            if first == 0:
-                for s in range(0, LOAD_SLICES, UNIT):
-                    nc.sync.dma_start(out=z_in[:, s : s + UNIT, :], in_=s_z2[:, s : s + UNIT, :])
-                c_codes, c_planes = load_weight(c_w3_words, c_w3_scales, "c_w")
-                s_codes, s_planes = load_weight(s_w3_words, s_w3_scales, "s_w")
-                units[0]["codes"] = c_codes
-                units[0]["planes"] = c_planes
-            else:
-                nc.sync.dma_start(out=z_in[:], in_=s_z2[:, first : first + LOAD_SLICES, :])
-            for s in range(0, LOAD_SLICES, UNIT):
-                units.append(
-                    dict(
-                        rows=[z_in[:, s + i, :] for i in range(UNIT)],
-                        gain=s_gain,
-                        shift=s_shift,
-                        codes=s_codes,
-                        planes=s_planes,
-                        first_slice=first + s,
-                        parity=len(units) % 2,
-                        squares=len(units) > 4 and len(units) % 2 == 1,
-                    )
+            loads.append(z_pool.tile([P, LOAD_SLICES, D], BF16, name="z_in"))
+        for first in range(0, 8, UNIT):
+            s = first % LOAD_SLICES
+            nc.sync.dma_start(
+                out=loads[first // LOAD_SLICES][:, s : s + UNIT, :], in_=s_z2[:, first : first + UNIT, :]
+            )
+        c_codes, c_planes = load_weight(c_w3_words, c_w3_scales, "c_w")
+        s_codes, s_planes = load_weight(s_w3_words, s_w3_scales, "s_w")
+        for first in range(8, S, LOAD_SLICES):
+            nc.sync.dma_start(out=loads[first // LOAD_SLICES][:], in_=s_z2[:, first : first + LOAD_SLICES, :])
+        units = [
+            dict(rows=[c_z[:]], gain=c_gain, shift=c_shift, codes=c_codes, planes=c_planes, first_slice=None, squares=False)
+        ]
+        for first in range(0, S, UNIT):
+            z_in = loads[first // LOAD_SLICES]
+            units.append(
+                dict(
+                    rows=[z_in[:, first % LOAD_SLICES + i, :] for i in range(UNIT)],
+                    gain=s_gain,
+                    shift=s_shift,
+                    codes=s_codes,
+                    planes=s_planes,
+                    first_slice=first,
+                    parity=len(units) % 2,
+                    squares=len(units) > 4 and len(units) % 3 > 0,
                 )
+            )
 
         ident = const.tile([P, P], BF16, name="ident")
         make_identity(nc, ident[:])
@@ -246,6 +250,11 @@ def tile_cgblock_pb_t_kernel(
             unit["grouped"] = [grouped]
             copy_rows(nc.scalar.copy, grouped[:], chunks_of(unit, s))
 
+        def regroup_second(unit, s, copy):
+            second = port_pool.tile([P, PASSES * B, PACK], BF16, name="second", align_bytes=64)
+            unit["grouped"].append(second)
+            copy_rows(copy, second[:], chunks_of(unit, s))
+
         def regroup_on_gpsimd(unit, s):
             second = port_pool.tile([P, PASSES * B, PACK], BF16, name="second", align_bytes=64)
             unit["grouped"].append(second)
@@ -276,11 +285,6 @@ def tile_cgblock_pb_t_kernel(
 
         def relu_on_scalar(out, in_):
             nc.scalar.activation(out=out, in_=in_, func=FUNC.Relu)
-
-        def regroup_with_relu(unit, s):
-            second = port_pool.tile([P, PASSES * B, PACK], BF16, name="second", align_bytes=64)
-            unit["grouped"].append(second)
-            copy_rows(relu_on_scalar, second[:], chunks_of(unit, s))
 
         def quantise(unit, s):
             if "h_codes" not in unit:
@@ -322,20 +326,18 @@ def tile_cgblock_pb_t_kernel(
                 unit["gated"] = gated
 
         def finish_last(unit):
-            pooled = const.tile([P, UNIT, N], F32, name="pooled")
+            gated = out_pool.tile(every_slice, F32, name="gated")
             result = result_pool.tile(every_slice, F32, name="result")
+            pooled = const.tile([P, UNIT + 2, N], F32, name="pooled")
             nc.vector.tensor_tensor(out=pooled[:, 0], in0=best[:, 0, :], in1=best[:, 1, :], op=ALU.max)
-            finish_first(unit)
             for s in range(UNIT):
-                nc.vector.tensor_tensor(
-                    out=result[:, s, :], in0=unit["gated"][:, s, :], in1=gated_bias[:], op=ALU.add
-                )
+                nc.vector.tensor_tensor(out=gated[:, s, :], in0=unit["acc"][:, s, :], in1=gate[:], op=ALU.mult)
+            for s in range(UNIT):
+                nc.vector.tensor_tensor(out=pooled[:, s + 1], in0=pooled[:, s], in1=gated[:, s, :], op=ALU.max)
+                nc.vector.tensor_tensor(out=result[:, s, :], in0=gated[:, s, :], in1=gated_bias[:], op=ALU.add)
                 nc.sync.dma_start(out=out_0[:, unit["first_slice"] + s, :], in_=result[:, s, :])
-                nc.vector.tensor_tensor(
-                    out=pooled[:, 1 - s], in0=pooled[:, s], in1=unit["gated"][:, s, :], op=ALU.max
-                )
-            nc.vector.tensor_tensor(out=pooled[:, 1], in0=pooled[:, 0], in1=gated_bias[:], op=ALU.add)
-            nc.sync.dma_start(out=out_1, in_=pooled[:, 1])
+            nc.vector.tensor_tensor(out=pooled[:, UNIT + 1], in0=pooled[:, UNIT], in1=gated_bias[:], op=ALU.add)
+            nc.sync.dma_start(out=out_1, in_=pooled[:, UNIT + 1])
 
         def finish_second(unit, engine):
             first_slice = unit["first_slice"]
@@ -417,7 +419,7 @@ def tile_cgblock_pb_t_kernel(
         multiply(previous, 1)
         finish_second(first, nc.vector)
         finish_third(first)
-        regroup_with_relu(final, 1)
+        regroup_second(final, 1, relu_on_scalar)
         finish_second(before, nc.vector)
         finish_third(before)
         finish_first(previous)
@@ -425,6 +427,6 @@ def tile_cgblock_pb_t_kernel(
         multiply(final, 0)
         quantise(final, 1)
         multiply(final, 1)
-        finish_second(previous, nc.vector)
         finish_third(previous)
+        finish_second(previous, nc.vector)
         finish_last(final)

from contextlib import ExitStack

import concourse.mybir as mybir
from concourse.masks import make_identity

F32 = mybir.dt.float32
BF16 = mybir.dt.bfloat16
I32 = mybir.dt.int32
U32 = mybir.dt.uint32
U8 = mybir.dt.uint8
FP8X4 = mybir.dt.float8_e4m3fn_x4
ALU = mybir.AluOpType
FUNC = mybir.ActivationFunctionType

P = 128
B, S, D, N = 128, 64, 1024, 256
EPS = 1e-5
PACK = 4
PASSES = D // (P * PACK)
CHUNKS = PASSES * PACK
UNIT = 2
LOAD_SLICES = 4
QUADRANTS = 4
GPSIMD_ROWS = 224
RUN = 8

FLOPS = 2 * (B * S + B) * D * N


def tile_cgblock_pb_t_kernel(
    tc,
    s_z2,
    c_z2,
    s_g2,
    s_be2,
    s_w3_words,
    s_w3_scales,
    s_b3,
    c_g2,
    c_be2,
    c_w3_words,
    c_w3_scales,
    c_b3,
    out_0,
    out_1,
):
    nc = tc.nc
    with ExitStack() as ctx:
        const = ctx.enter_context(tc.tile_pool(name="const", bufs=1))
        z_pool = ctx.enter_context(tc.tile_pool(name="z", bufs=S // LOAD_SLICES))
        small = ctx.enter_context(tc.tile_pool(name="small", bufs=3))
        work_pool = ctx.enter_context(tc.tile_pool(name="work", bufs=2))
        port_pool = ctx.enter_context(tc.tile_pool(name="port", bufs=1))
        out_pool = ctx.enter_context(tc.tile_pool(name="out", bufs=3))
        result_pool = ctx.enter_context(tc.tile_pool(name="results", bufs=8))
        zt_pool = ctx.enter_context(tc.psum_pool(name="zt", bufs=6))
        mean_pool = ctx.enter_context(tc.psum_pool(name="mean", bufs=1))
        acc_pool = ctx.enter_context(tc.psum_pool(name="acc", bufs=1))
        ctx.enter_context(tc.manual_schedule())

        def load_weight(words, scales, label):
            codes = const.tile([P, PASSES, N], U32, name=label + "_codes", align_bytes=64)
            nc.sync.dma_start(
                out=codes[:].bitcast(I32),
                in_=words.rearrange("g p n t -> p g (n t)").bitcast(I32),
            )
            planes = const.tile([P, PASSES, N], U8, name=label + "_planes", align_bytes=64)
            nc.vector.memset(planes[:].bitcast(I32), 0)
            for quad in range(QUADRANTS):
                nc.sync.dma_start(
                    out=planes[32 * quad : 32 * quad + 4].bitcast(I32),
                    in_=scales[:, 4 * quad : 4 * quad + 4, :].rearrange("g r n -> r g n").bitcast(I32),
                )
            return codes, planes

        def load_by_chunk(vector, label):
            by_chunk = const.tile([P, PASSES, PACK], BF16, name=label)
            nc.scalar.dma_start(out=by_chunk[:], in_=vector.rearrange("(g p t) -> p g t", g=PASSES, t=PACK))
            return by_chunk[:].rearrange("p g t -> p (g t)")

        def load_on_all_partitions(vector, label):
            rows = const.tile([P, N], BF16, name=label)
            nc.scalar.dma_start(out=rows[:], in_=vector.partition_broadcast(P))
            return rows

        c_z = const.tile([P, D], BF16, name="c_z")
        nc.sync.dma_start(out=c_z[:], in_=c_z2)
        c_gain = load_by_chunk(c_g2, "c_gain")
        c_shift = load_by_chunk(c_be2, "c_shift")
        s_gain = load_by_chunk(s_g2, "s_gain")
        s_shift = load_by_chunk(s_be2, "s_shift")
        c_bias = load_on_all_partitions(c_b3, "c_bias")
        s_bias = load_on_all_partitions(s_b3, "s_bias")

        loads = []
        for first in range(0, S, LOAD_SLICES):
            loads.append(z_pool.tile([P, LOAD_SLICES, D], BF16, name="z_in"))
        for first in range(0, 8, UNIT):
            s = first % LOAD_SLICES
            nc.sync.dma_start(
                out=loads[first // LOAD_SLICES][:, s : s + UNIT, :], in_=s_z2[:, first : first + UNIT, :]
            )
        c_codes, c_planes = load_weight(c_w3_words, c_w3_scales, "c_w")
        s_codes, s_planes = load_weight(s_w3_words, s_w3_scales, "s_w")
        for first in range(8, S, LOAD_SLICES):
            nc.sync.dma_start(out=loads[first // LOAD_SLICES][:], in_=s_z2[:, first : first + LOAD_SLICES, :])
        units = [
            dict(rows=[c_z[:]], gain=c_gain, shift=c_shift, codes=c_codes, planes=c_planes, first_slice=None, squares=False)
        ]
        for first in range(0, S, UNIT):
            z_in = loads[first // LOAD_SLICES]
            units.append(
                dict(
                    rows=[z_in[:, first % LOAD_SLICES + i, :] for i in range(UNIT)],
                    gain=s_gain,
                    shift=s_shift,
                    codes=s_codes,
                    planes=s_planes,
                    first_slice=first,
                    parity=len(units) % 2,
                    squares=len(units) > 4 and len(units) % 3 > 0,
                )
            )

        ident = const.tile([P, P], BF16, name="ident")
        make_identity(nc, ident[:])
        mean_column = const.tile([P, 1], BF16, name="mean_column")
        nc.vector.memset(mean_column[:], 1.0 / B)
        eps = const.tile([P, 1], F32, name="eps")
        nc.vector.memset(eps[:], EPS)
        warm = const.tile([P, 1], F32, name="warm")
        nc.scalar.activation(out=warm[:], in_=eps[:], func=FUNC.Sqrt)
        gate = const.tile([P, N], F32, name="gate")
        gated_bias = const.tile([P, N], F32, name="gated_bias")
        best = const.tile([P, UNIT, N], F32, name="best")

        means = mean_pool.tile([P, 2, 2], F32, name="means")

        def transpose(unit, s):
            if s == 0:
                unit["banks"] = []
                stats = small.tile([P, UNIT, CHUNKS, 3], F32, name="stats")
                unit["stats"] = stats
            zt = zt_pool.tile([P, CHUNKS, B], BF16, name="zt")
            by_byte = unit["rows"][s].rearrange("b (g p t) -> b g t p", g=PASSES, t=PACK)
            for g in range(PASSES):
                for t in range(PACK):
                    nc.tensor.transpose(zt[:, g * PACK + t, :], by_byte[:, g, t, :], ident[:])
            if s == 0 and unit["squares"]:
                for i in range(2):
                    nc.tensor.matmul(
                        means[:, unit["parity"], i : i + 1],
                        lhsT=by_byte[:, 1, 2 + i, :],
                        rhs=mean_column[:],
                        start=True,
                        stop=True,
                    )
            unit["banks"].append(zt)

        def fetch_means(unit, s):
            if unit["squares"]:
                nc.scalar.copy(out=unit["stats"][:, s, 6:8, 1], in_=means[:, unit["parity"], :])

        def square(unit, s):
            if unit["squares"]:
                junk = work_pool.tile([P, 2, B], BF16, name="junk")
                for i in range(2):
                    nc.scalar.activation(
                        out=junk[:, i, :],
                        in_=unit["banks"][s][:, 6 + i, :],
                        func=FUNC.Square,
                        bias=unit["stats"][:, s, 6 + i, 1:2],
                        scale=-1.0,
                        accum_out=unit["stats"][:, s, 6 + i, 2:3],
                    )

        def statistics(unit, s, j):
            if s == 0 and j == 6 and unit["squares"]:
                return
            nc.vector.bn_stats(
                out=unit["stats"][:, s, j : j + 2, :].rearrange("p e v -> p (e v)"),
                in_=unit["banks"][s][:, j : j + 2, :].rearrange("p e b -> p b e"),
            )

        def deviation(unit):
            n = len(unit["rows"])
            std = small.tile([P, UNIT, CHUNKS], F32, name="std")
            nc.scalar.activation(
                out=std[:, :n], in_=unit["stats"][:, :n, :, 2], func=FUNC.Sqrt, bias=eps[:], scale=1.0 / B
            )
            unit["std"] = std

        def inverse_deviation(unit):
            n = len(unit["rows"])
            rstd = small.tile([P, UNIT, CHUNKS], F32, name="rstd")
            nc.vector.reciprocal(out=rstd[:, :n], in_=unit["std"][:, :n])
            unit["rstd"] = rstd

        def slope(unit):
            n = len(unit["rows"])
            slopes = small.tile([P, UNIT, CHUNKS], F32, name="slopes")
            nc.vector.tensor_tensor(
                out=slopes[:, :n],
                in0=unit["rstd"][:, :n],
                in1=unit["gain"].unsqueeze(1).to_broadcast([P, n, CHUNKS]),
                op=ALU.mult,
            )
            unit["slopes"] = slopes

        def slope_times_mean(unit):
            n = len(unit["rows"])
            scaled_mean = small.tile([P, UNIT, CHUNKS], F32, name="scaled_mean")
            nc.vector.tensor_tensor(
                out=scaled_mean[:, :n], in0=unit["slopes"][:, :n], in1=unit["stats"][:, :n, :, 1], op=ALU.mult
            )
            unit["scaled_mean"] = scaled_mean

        def offset(unit):
            n = len(unit["rows"])
            offsets = small.tile([P, UNIT, CHUNKS], F32, name="offsets")
            nc.vector.tensor_tensor(
                out=offsets[:, :n],
                in0=unit["shift"].unsqueeze(1).to_broadcast([P, n, CHUNKS]),
                in1=unit["scaled_mean"][:, :n],
                op=ALU.subtract,
            )
            unit["offsets"] = offsets

        def normalise(unit, s, chunks=range(CHUNKS)):
            if (s, chunks[0]) == (0, 0):
                h = work_pool.tile([P, UNIT, PACK, PASSES, B], BF16, name="h")
                unit["h"] = h
            for j in chunks:
                nc.scalar.activation(
                    out=unit["h"][:, s, j % PACK, j // PACK, :],
                    in_=unit["banks"][s][:, j, :],
                    func=FUNC.Relu,
                    bias=unit["offsets"][:, s, j : j + 1],
                    scale=unit["slopes"][:, s, j : j + 1],
                )

        def chunks_of(unit, s):
            return unit["h"][:, s].rearrange("p t g b -> p t (g b)")

        def copy_rows(copy, out, in_):
            copy(out=out.rearrange("p (c i) t -> p c t i", i=RUN), in_=in_.rearrange("p t (c i) -> p c t i", i=RUN))

        def regroup_first(unit, s):
            grouped = work_pool.tile([P, PASSES * B, PACK], BF16, name="grouped", align_bytes=64)
            unit["grouped"] = [grouped]
            copy_rows(nc.scalar.copy, grouped[:], chunks_of(unit, s))

        def regroup_second(unit, s, copy):
            second = port_pool.tile([P, PASSES * B, PACK], BF16, name="second", align_bytes=64)
            unit["grouped"].append(second)
            copy_rows(copy, second[:], chunks_of(unit, s))

        def regroup_on_gpsimd(unit, s):
            second = port_pool.tile([P, PASSES * B, PACK], BF16, name="second", align_bytes=64)
            unit["grouped"].append(second)
            nc.gpsimd.tensor_scalar(
                out=second[:, :GPSIMD_ROWS, :],
                in0=chunks_of(unit, s)[:, :, :GPSIMD_ROWS].rearrange("p t r -> p r t"),
                scalar1=1.0,
                scalar2=0.0,
                op0=ALU.mult,
                op1=ALU.add,
            )

        def regroup_rest(unit, s):
            copy_rows(
                nc.scalar.copy, unit["grouped"][s][:, GPSIMD_ROWS:, :], chunks_of(unit, s)[:, :, GPSIMD_ROWS:]
            )

        def normalise_on_vector(unit, s):
            for j in range(CHUNKS):
                nc.vector.tensor_scalar(
                    out=unit["h"][:, s, j % PACK, j // PACK, :],
                    in0=unit["banks"][s][:, j, :],
                    scalar1=unit["slopes"][:, s, j : j + 1],
                    scalar2=unit["offsets"][:, s, j : j + 1],
                    op0=ALU.mult,
                    op1=ALU.add,
                )

        def relu_on_scalar(out, in_):
            nc.scalar.activation(out=out, in_=in_, func=FUNC.Relu)

        def quantise(unit, s):
            if "h_codes" not in unit:
                h_codes = work_pool.tile([P, UNIT, PASSES, B], U32, name="h_codes", align_bytes=64)
                h_planes = work_pool.tile([P, UNIT, PASSES, B], U8, name="h_planes", align_bytes=64)
                unit["h_codes"] = h_codes
                unit["h_planes"] = h_planes
            nc.vector.quantize_mx(
                out=unit["h_codes"][:, s].rearrange("p g b -> p (g b)").bitcast(FP8X4),
                scales=unit["h_planes"][:, s].rearrange("p g b -> p (g b)"),
                in_=unit["grouped"][s][:].rearrange("p r t -> p (r t)"),
            )

        def multiply(unit, s):
            if "acc" not in unit:
                acc = acc_pool.tile([P, UNIT, N], F32, name="acc")
                unit["acc"] = acc
            for g in range(PASSES):
                nc.tensor.matmul_mx(
                    out=unit["acc"][:, s, :],
                    lhsT=unit["h_codes"][:, s, g, :].bitcast(FP8X4),
                    lhsT_scale=unit["h_planes"][:, s, g, :],
                    rhs=unit["codes"][:, g, :].bitcast(FP8X4),
                    rhs_scale=unit["planes"][:, g, :],
                    start=(g == 0),
                    stop=(g == PASSES - 1),
                )

        every_slice = [P, UNIT, N]

        def finish_first(unit):
            if unit["first_slice"] is None:
                nc.vector.tensor_tensor(out=gate[:], in0=unit["acc"][:, 0, :], in1=c_bias[:], op=ALU.add)
            else:
                gated = out_pool.tile(every_slice, F32, name="gated")
                nc.vector.tensor_tensor(
                    out=gated[:], in0=unit["acc"][:], in1=gate[:].unsqueeze(1).to_broadcast(every_slice), op=ALU.mult
                )
                unit["gated"] = gated

        def finish_last(unit):
            gated = out_pool.tile(every_slice, F32, name="gated")
            result = result_pool.tile(every_slice, F32, name="result")
            pooled = const.tile([P, UNIT + 2, N], F32, name="pooled")
            nc.vector.tensor_tensor(out=pooled[:, 0], in0=best[:, 0, :], in1=best[:, 1, :], op=ALU.max)
            for s in range(UNIT):
                nc.vector.tensor_tensor(out=gated[:, s, :], in0=unit["acc"][:, s, :], in1=gate[:], op=ALU.mult)
            for s in range(UNIT):
                nc.vector.tensor_tensor(out=pooled[:, s + 1], in0=pooled[:, s], in1=gated[:, s, :], op=ALU.max)
                nc.vector.tensor_tensor(out=result[:, s, :], in0=gated[:, s, :], in1=gated_bias[:], op=ALU.add)
                nc.sync.dma_start(out=out_0[:, unit["first_slice"] + s, :], in_=result[:, s, :])
            nc.vector.tensor_tensor(out=pooled[:, UNIT + 1], in0=pooled[:, UNIT], in1=gated_bias[:], op=ALU.add)
            nc.sync.dma_start(out=out_1, in_=pooled[:, UNIT + 1])

        def finish_second(unit, engine):
            first_slice = unit["first_slice"]
            if first_slice is None:
                nc.vector.tensor_tensor(out=gated_bias[:], in0=gate[:], in1=s_bias[:], op=ALU.mult)
            else:
                result = result_pool.tile(every_slice, F32, name="result")
                engine.tensor_tensor(
                    out=result[:],
                    in0=unit["gated"][:],
                    in1=gated_bias[:].unsqueeze(1).to_broadcast(every_slice),
                    op=ALU.add,
                )
                nc.sync.dma_start(out=out_0[:, first_slice : first_slice + UNIT, :], in_=result[:])

        def finish_third(unit):
            first_slice = unit["first_slice"]
            if first_slice is None:
                return
            if first_slice == 0:
                nc.vector.tensor_copy(out=best[:], in_=unit["gated"][:])
            else:
                nc.vector.tensor_tensor(out=best[:], in0=best[:], in1=unit["gated"][:], op=ALU.max)

        def do(stage, u, *where):
            if 0 <= u < len(units) and (len(where) == 0 or where[0] < len(units[u]["rows"])):
                stage(units[u], *where)

        last = len(units) - 1
        do(transpose, 0, 0)
        for k in range(-1, last + 1):
            do(transpose, k + 1, 1)
            reads = [(k, 1, j) for j in range(0, CHUNKS, 2)] + [(k + 1, 0, j) for j in range(0, CHUNKS, 2)]
            if k <= 2:
                reads = reads[: CHUNKS // 2]
            for read in reads:
                do(statistics, *read)
            if k - 2 > 0:
                do(regroup_on_gpsimd, k - 2, 1)
            do(lambda unit: finish_second(unit, nc.gpsimd), k - 4)
            if k <= 2:
                do(statistics, k + 1, 0, 0)
                do(statistics, k + 1, 0, 2)
            do(fetch_means, k + 1, 0)
            do(normalise, k - 1, 0)
            do(transpose, k + 2, 0)
            do(deviation, k)
            do(regroup_rest, k - 2, 1)
            do(normalise, k - 1, 1)
            do(regroup_first, k - 1, 0)
            do(square, k + 1, 0)
            if k > 2:
                do(inverse_deviation, k)
            do(finish_first, k - 3)
            if k <= 2:
                do(inverse_deviation, k)
                do(statistics, k + 1, 0, 4)
            do(slope, k)
            do(finish_third, k - 4)
            if k <= 2:
                do(statistics, k + 1, 0, 6)
            do(slope_times_mean, k)
            do(quantise, k - 2, 1)
            do(multiply, k - 2, 1)
            do(offset, k)
            do(quantise, k - 2, 0)
            do(multiply, k - 2, 0)

        first, before, previous, final = units[-4:]
        regroup_on_gpsimd(previous, 1)
        regroup_rest(previous, 1)
        normalise(final, 0)
        regroup_first(final, 0)
        normalise_on_vector(final, 1)
        finish_first(before)
        quantise(previous, 0)
        multiply(previous, 0)
        quantise(previous, 1)
        multiply(previous, 1)
        finish_second(first, nc.vector)
        finish_third(first)
        regroup_second(final, 1, relu_on_scalar)
        finish_second(before, nc.vector)
        finish_third(before)
        finish_first(previous)
        quantise(final, 0)
        multiply(final, 0)
        quantise(final, 1)
        multiply(final, 1)
        finish_third(previous)
        finish_second(previous, nc.vector)
        finish_last(final)
